import numpy as np
import ml_dtypes


def mxq(x, axis, fmt="e4m3"):
    dtype, down = {"e4m3": (ml_dtypes.float8_e4m3fn, 7), "e5m2": (ml_dtypes.float8_e5m2, 14)}[fmt]
    v = np.moveaxis(np.asarray(x, np.float32).astype(ml_dtypes.bfloat16).astype(np.float64), axis, -1)
    blocks = v.reshape(v.shape[:-1] + (-1, 32))
    amax = np.abs(blocks).max(-1, keepdims=True)
    byte = np.maximum(np.where(amax > 0, np.frexp(amax)[1] - 1 + 127, 0) - down, 1)
    scale = np.exp2(byte - 127.0)
    codes = (blocks / scale).astype(np.float32).astype(dtype).astype(np.float64)
    return np.moveaxis((codes * scale).reshape(v.shape), -1, axis)


WIDE = False


def mx_kscale(k):
    if not WIDE:
        return np.ones(k)
    levels = np.array([10, -10, 5, -5, 0])
    a = np.random.permutation(np.resize(levels, k // 512 * 4)).reshape(k // 512, 4)
    idx = np.arange(k)
    return np.exp2(a[idx // 512, idx % 128 // 32])


BF16 = ml_dtypes.bfloat16


def bf(x):
    return np.asarray(x, np.float32).astype(BF16)


def f64(x):
    return np.asarray(x).astype(np.float64)


E2M1 = np.array([0.0, 0.5, 1.0, 1.5, 2.0, 3.0, 4.0, 6.0, -0.0, -0.5, -1.0, -1.5, -2.0, -3.0, -4.0, -6.0])


def pack_weight(w, fmt):
    k, n = w.shape
    w = f64(bf(w)).reshape(k // 32, 32, n)
    amax = np.abs(w).max(1)
    if fmt == "e4m3":
        byte = np.frexp(amax)[1] - 1 + 127 - 7
    else:
        mant, ex = np.frexp(amax / 6.0)
        byte = np.where(mant > 0.5, ex, ex - 1) + 127
    byte = np.clip(np.where(amax > 0, byte, 1), 1, 254)
    scaled = (w * np.exp2(127.0 - byte)[:, None, :]).reshape(k, n).astype(np.float32)
    by_word = np.ascontiguousarray(scaled.reshape(k // 512, 128, 4, n).transpose(0, 1, 3, 2))
    if fmt == "e4m3":
        words = by_word.astype(ml_dtypes.float8_e4m3fn).view(np.uint8)
    else:
        c = by_word.astype(ml_dtypes.float4_e2m1fn).view(np.uint8) & 0xF
        words = c[..., 0::2] | (c[..., 1::2] << 4)
    return np.ascontiguousarray(words), np.ascontiguousarray(byte.astype(np.uint8).reshape(k // 512, 16, n))


def unpack_weight(words, scales, fmt):
    g, p, n, _ = words.shape
    if fmt == "e4m3":
        vals = np.ascontiguousarray(words).view(ml_dtypes.float8_e4m3fn).astype(np.float64)
    else:
        nib = np.empty((g, p, n, 4), np.uint8)
        nib[..., 0::2] = words & 0xF
        nib[..., 1::2] = words >> 4
        vals = E2M1[nib]
    vals = vals * np.repeat(np.exp2(scales.astype(np.float64) - 127.0), 8, axis=1)[..., None]
    return vals.transpose(0, 1, 3, 2).reshape(g * 512, n)

def pack4(w):
    words, scales = pack_weight(w, "e2m1")
    return words.reshape(words.shape[0], 128, -1), scales


def unpack4(words, scales):
    return unpack_weight(words.reshape(words.shape[0], 128, -1, 2), scales, "e2m1")


B, CIN, P, COUT, W, H, HEADS = 16, 1024, 512, 256, 16, 32, 4
N = W * H
EPS = 1e-5


def bn(y, g, b, m, v):
    return (y - f64(m)[None, :, None]) * (f64(g) / np.sqrt(f64(v) + EPS))[None, :, None] + f64(b)[None, :, None]


def setup_inputs():
    s, t = mx_kscale(P), mx_kscale(CIN)
    inp = {}
    inp["h_attn"] = bf(np.maximum(np.random.standard_normal((B, P, N)), 0.0) * s[None, :, None])
    inp["x"] = bf(np.random.standard_normal((B, CIN, N)) * t[None, :, None])
    conv3_w = np.random.standard_normal((COUT, P)) * 1.5 / np.sqrt(P) / s[None, :]
    inp["conv3_w_words"], inp["conv3_w_scales"] = pack4(conv3_w.T)
    inp["bn3_g"] = bf(np.random.uniform(0.5, 1.5, COUT))
    inp["bn3_b"] = bf(np.random.standard_normal(COUT) * 0.3)
    inp["bn3_m"] = bf(np.random.standard_normal(COUT) * 0.3)
    inp["bn3_v"] = bf(np.random.uniform(0.5, 1.5, COUT))
    sc_w = np.random.standard_normal((COUT, CIN)) / np.sqrt(CIN) / t[None, :]
    inp["sc_w_words"], inp["sc_w_scales"] = pack4(sc_w.T)
    inp["sc_b"] = bf(np.random.standard_normal(COUT) * 0.3)
    inp["scbn_g"] = bf(np.random.uniform(0.5, 1.5, COUT))
    inp["scbn_b"] = bf(np.random.standard_normal(COUT) * 0.3)
    inp["scbn_m"] = bf(np.random.standard_normal(COUT) * 0.3)
    inp["scbn_v"] = bf(np.random.uniform(0.5, 1.5, COUT))
    return inp


def reference(h_attn, x, conv3_w_words, conv3_w_scales, bn3_g, bn3_b, bn3_m, bn3_v, sc_w_words, sc_w_scales, sc_b, scbn_g, scbn_b, scbn_m, scbn_v):
    main = bn(unpack4(conv3_w_words, conv3_w_scales).T @ mxq(f64(h_attn), 1, "e4m3"), bn3_g, bn3_b, bn3_m, bn3_v)
    short = (unpack4(sc_w_words, sc_w_scales).T @ mxq(f64(x), 1, "e4m3")) + f64(sc_b)[None, :, None]
    short = bn(short, scbn_g, scbn_b, scbn_m, scbn_v)
    return np.maximum(main + short, 0.0)

@@ -1,0 +1,224 @@
+from contextlib import ExitStack
+
+import concourse.mybir as mybir
+from concourse.masks import make_identity
+
+F32 = mybir.dt.float32
+BF16 = mybir.dt.bfloat16
+I32 = mybir.dt.int32
+U32 = mybir.dt.uint32
+U8 = mybir.dt.uint8
+FP8X4 = mybir.dt.float8_e4m3fn_x4
+FP4X4 = mybir.dt.float4_e2m1fn_x4
+ALU = mybir.AluOpType
+ACT = mybir.ActivationFunctionType
+
+P = 128
+PACK = 4
+BATCH = 16
+C_MAIN = 512
+C_SHORT = 1024
+C_OUT = 256
+M_TILES = C_OUT // P
+POS = 512
+PASSES = (C_MAIN + C_SHORT) // (P * PACK)
+EPS = 1e-5
+
+FLOPS = 2 * BATCH * C_OUT * (C_MAIN + C_SHORT) * POS
+
+VECTOR_COLS = 224
+RUN = 4
+LOOKAHEAD = 5
+LAG = 2
+
+
+def tile_bottleneck_transformer_pb_t_kernel(
+    tc,
+    h_attn,
+    x,
+    conv3_w_words,
+    conv3_w_scales,
+    bn3_g,
+    bn3_b,
+    bn3_m,
+    bn3_v,
+    sc_w_words,
+    sc_w_scales,
+    sc_b,
+    scbn_g,
+    scbn_b,
+    scbn_m,
+    scbn_v,
+    out,
+):
+    nc = tc.nc
+    with ExitStack() as ctx:
+        const = ctx.enter_context(tc.tile_pool(name="const", bufs=1))
+        raw = ctx.enter_context(tc.tile_pool(name="raw", bufs=LOOKAHEAD + 1))
+        stage = ctx.enter_context(tc.tile_pool(name="stage", bufs=4))
+        result = ctx.enter_context(tc.tile_pool(name="result", bufs=3))
+        psum = ctx.enter_context(tc.psum_pool(name="psum", bufs=2))
+
+        w_words = const.tile([P, PASSES, 2 * C_OUT], U8, align_bytes=64)
+        w_scales = const.tile([P, PASSES, C_OUT], U8, align_bytes=64)
+        nc.vector.memset(w_scales[:].rearrange("p s n -> p (s n)").bitcast(I32), 0)
+
+        def load_weight(words, scales, first_pass, passes):
+            mine = slice(first_pass, first_pass + passes)
+            nc.sync.dma_start(
+                out=w_words[:, mine, :].bitcast(I32),
+                in_=words.rearrange("g p n -> p g n").bitcast(I32),
+            )
+            for quadrant in range(4):
+                nc.sync.dma_start(
+                    out=w_scales[32 * quadrant : 32 * quadrant + 4, mine, :].bitcast(I32),
+                    in_=scales[:, 4 * quadrant : 4 * quadrant + 4, :]
+                    .rearrange("g r n -> r g n")
+                    .bitcast(I32),
+                )
+
+        def load_batch(b):
+            h_raw = raw.tile([P, PACK, POS], BF16)
+            nc.sync.dma_start(out=h_raw[:], in_=h_attn[b].rearrange("(p j) w -> p j w", j=PACK))
+            x_raw = raw.tile([P, C_SHORT // (P * PACK), PACK, POS], BF16)
+            nc.sync.dma_start(
+                out=x_raw[:], in_=x[b].rearrange("(g p j) w -> p g j w", p=P, j=PACK)
+            )
+            return [h_raw[:], x_raw[:, 0], x_raw[:, 1]]
+
+        bn_rows = const.tile([P, P], BF16)
+        nc.vector.memset(bn_rows[:], 0.0)
+        identity = const.tile([P, P], BF16)
+        make_identity(nc, identity[:])
+        vectors = [bn3_v, scbn_v, bn3_g, scbn_g, bn3_m, scbn_m, bn3_b, scbn_b, sc_b]
+        for v, vector in enumerate(vectors):
+            nc.gpsimd.dma_start(
+                out=bn_rows[M_TILES * v : M_TILES * (v + 1), :],
+                in_=vector.rearrange("(m c) -> m c", m=M_TILES),
+            )
+
+        ones = const.tile([P, 1], F32)
+        nc.vector.memset(ones[:], 1.0)
+        warm = const.tile([P, 1], F32)
+        nc.scalar.activation(out=warm[:], in_=ones[:], func=ACT.Sqrt)
+
+        scale = const.tile([P, 2 * M_TILES], F32)
+        offset = const.tile([P, M_TILES], F32)
+
+        def fold_batch_norms():
+            cols_ps = psum.tile([P, P], BF16, tag="main0")
+            nc.tensor.transpose(cols_ps[:], bn_rows[:], identity[:])
+            cols = const.tile([P, M_TILES * len(vectors)], F32)
+            nc.vector.tensor_copy(out=cols[:], in_=cols_ps[:, 0 : M_TILES * len(vectors)])
+            var, gain, mean, shift = [cols[:, 4 * i : 4 * i + 4] for i in range(4)]
+            bias = cols[:, 16:18]
+            var_eps = const.tile([P, 4], F32)
+            nc.vector.tensor_scalar_add(out=var_eps[:], in0=var, scalar1=EPS)
+            std = const.tile([P, 4], F32)
+            nc.scalar.activation(out=std[:], in_=var_eps[:], func=ACT.Sqrt)
+            rstd = const.tile([P, 4], F32)
+            nc.vector.reciprocal(out=rstd[:], in_=std[:])
+            nc.vector.tensor_mul(out=scale[:], in0=gain, in1=rstd[:])
+            centre = const.tile([P, 4], F32)
+            nc.vector.tensor_copy(out=centre[:, 0:2], in_=mean[:, 0:2])
+            nc.vector.tensor_sub(out=centre[:, 2:4], in0=mean[:, 2:4], in1=bias)
+            scaled_centre = const.tile([P, 4], F32)
+            nc.vector.tensor_mul(out=scaled_centre[:], in0=centre[:], in1=scale[:])
+            both = const.tile([P, 4], F32)
+            nc.vector.tensor_sub(out=both[:], in0=shift, in1=scaled_centre[:])
+            nc.vector.tensor_add(out=offset[:], in0=both[:, 0:2], in1=both[:, 2:4])
+
+        def regroup(rows):
+            grouped = stage.tile([P, POS, PACK], BF16, align_bytes=64)
+            for copy, cols in (
+                (nc.vector.tensor_copy, slice(0, VECTOR_COLS)),
+                (nc.scalar.copy, slice(VECTOR_COLS, POS)),
+            ):
+                copy(
+                    out=grouped[:, cols, :].rearrange("p (c i) j -> p c j i", i=RUN),
+                    in_=rows[:, :, cols].rearrange("p j (c i) -> p c j i", i=RUN),
+                )
+            return grouped
+
+        def quantise_and_multiply(grouped, s, accs):
+            codes = stage.tile([P, POS], U32, align_bytes=64)
+            scales = stage.tile([P, POS], U8, align_bytes=64)
+            nc.vector.quantize_mx(
+                out=codes[:].bitcast(FP8X4),
+                scales=scales[:],
+                in_=grouped[:].rearrange("p w j -> p (w j)"),
+            )
+            for m in range(M_TILES):
+                nc.tensor.matmul_mx(
+                    out=accs[m][:],
+                    lhsT=w_words[:, s, 2 * P * m : 2 * P * (m + 1)].bitcast(FP4X4),
+                    lhsT_scale=w_scales[:, s, P * m : P * (m + 1)],
+                    rhs=codes[:].bitcast(FP8X4),
+                    rhs_scale=scales[:],
+                    start=(s != 2),
+                    stop=(s != 1),
+                )
+
+        def finish_batch(b, main, short):
+            scaled_main = result.tile([P, M_TILES, POS], F32)
+            summed = result.tile([P, M_TILES, POS], F32)
+            rectified = result.tile([P, M_TILES, POS], F32)
+            for m in range(M_TILES):
+                nc.scalar.activation(
+                    out=scaled_main[:, m, :], in_=main[m][:], func=ACT.Copy, scale=scale[:, m : m + 1]
+                )
+            for m in range(M_TILES):
+                nc.vector.scalar_tensor_tensor(
+                    out=summed[:, m, :],
+                    in0=short[m][:],
+                    scalar=scale[:, M_TILES + m : M_TILES + m + 1],
+                    in1=scaled_main[:, m, :],
+                    op0=ALU.mult,
+                    op1=ALU.add,
+                )
+            for m in range(M_TILES):
+                nc.vector.tensor_scalar(
+                    out=rectified[:, m, :],
+                    in0=summed[:, m, :],
+                    scalar1=offset[:, m : m + 1],
+                    scalar2=0.0,
+                    op0=ALU.add,
+                    op1=ALU.max,
+                )
+            nc.sync.dma_start(out=out[b].rearrange("(m p) w -> p m w", p=P), in_=rectified[:])
+
+        rows_of = {}
+        grouped_of = {}
+        accs_of = {}
+        chunks = BATCH * PASSES
+
+        def step(n):
+            if n < chunks:
+                b, s = divmod(n, PASSES)
+                if s == 0 and b + LOOKAHEAD < BATCH:
+                    rows_of[b + LOOKAHEAD] = load_batch(b + LOOKAHEAD)
+                grouped_of[n] = regroup(rows_of[b][s])
+            if 1 <= n <= chunks:
+                b, s = divmod(n - 1, PASSES)
+                if s == 0:
+                    accs_of[b] = (
+                        [psum.tile([P, POS], F32, name="main%d" % m) for m in range(M_TILES)],
+                        [psum.tile([P, POS], F32, name="short%d" % m) for m in range(M_TILES)],
+                    )
+                quantise_and_multiply(grouped_of[n - 1], s, accs_of[b][min(s, 1)])
+            if n >= PASSES - 1 + LAG and (n - LAG) % PASSES == PASSES - 1:
+                b = (n - LAG) // PASSES
+                finish_batch(b, accs_of[b][0], accs_of[b][1])
+
+        rows_of[0] = load_batch(0)
+        load_weight(conv3_w_words, conv3_w_scales, 0, 1)
+        load_weight(sc_w_words, sc_w_scales, 1, 2)
+        for b in range(1, LOOKAHEAD):
+            rows_of[b] = load_batch(b)
+
+        first_finish = PASSES - 1 + LAG
+        for n in range(first_finish):
+            step(n)
+        fold_batch_norms()
+        for n in range(first_finish, chunks + LAG):
+            step(n)

@@ -29,7 +29,8 @@ FLOPS = 2 * BATCH * C_OUT * (C_MAIN + C_SHORT) * POS
 VECTOR_COLS = 224
 RUN = 4
 LOOKAHEAD = 5
-LAG = 2
+LAG = 4
+SCALAR_QUEUE_VECTORS = 5
 
 
 def tile_bottleneck_transformer_pb_t_kernel(
@@ -53,9 +54,11 @@ def tile_bottleneck_transformer_pb_t_kernel(
 ):
     nc = tc.nc
     with ExitStack() as ctx:
+        ctx.enter_context(tc.manual_schedule())
         const = ctx.enter_context(tc.tile_pool(name="const", bufs=1))
         raw = ctx.enter_context(tc.tile_pool(name="raw", bufs=LOOKAHEAD + 1))
-        stage = ctx.enter_context(tc.tile_pool(name="stage", bufs=4))
+        stage = ctx.enter_context(tc.tile_pool(name="stage", bufs=3))
+        quantised = ctx.enter_context(tc.tile_pool(name="quantised", bufs=8))
         result = ctx.enter_context(tc.tile_pool(name="result", bufs=3))
         psum = ctx.enter_context(tc.psum_pool(name="psum", bufs=2))
 
@@ -77,14 +80,20 @@ def tile_bottleneck_transformer_pb_t_kernel(
                     .bitcast(I32),
                 )
 
-        def load_batch(b):
+        rows_of = {}
+
+        def load_h(b):
             h_raw = raw.tile([P, PACK, POS], BF16)
             nc.sync.dma_start(out=h_raw[:], in_=h_attn[b].rearrange("(p j) w -> p j w", j=PACK))
+            rows_of[(b, 0)] = h_raw[:]
+
+        def load_x(b):
             x_raw = raw.tile([P, C_SHORT // (P * PACK), PACK, POS], BF16)
             nc.sync.dma_start(
                 out=x_raw[:], in_=x[b].rearrange("(g p j) w -> p g j w", p=P, j=PACK)
             )
-            return [h_raw[:], x_raw[:, 0], x_raw[:, 1]]
+            rows_of[(b, 1)] = x_raw[:, 0]
+            rows_of[(b, 2)] = x_raw[:, 1]
 
         bn_rows = const.tile([P, P], BF16)
         nc.vector.memset(bn_rows[:], 0.0)
@@ -92,7 +101,8 @@ def tile_bottleneck_transformer_pb_t_kernel(
         make_identity(nc, identity[:])
         vectors = [bn3_v, scbn_v, bn3_g, scbn_g, bn3_m, scbn_m, bn3_b, scbn_b, sc_b]
         for v, vector in enumerate(vectors):
-            nc.gpsimd.dma_start(
+            queue = nc.scalar if v < SCALAR_QUEUE_VECTORS else nc.gpsimd
+            queue.dma_start(
                 out=bn_rows[M_TILES * v : M_TILES * (v + 1), :],
                 in_=vector.rearrange("(m c) -> m c", m=M_TILES),
             )
@@ -106,8 +116,6 @@ def tile_bottleneck_transformer_pb_t_kernel(
         offset = const.tile([P, M_TILES], F32)
 
         def fold_batch_norms():
-            cols_ps = psum.tile([P, P], BF16, tag="main0")
-            nc.tensor.transpose(cols_ps[:], bn_rows[:], identity[:])
             cols = const.tile([P, M_TILES * len(vectors)], F32)
             nc.vector.tensor_copy(out=cols[:], in_=cols_ps[:, 0 : M_TILES * len(vectors)])
             var, gain, mean, shift = [cols[:, 4 * i : 4 * i + 4] for i in range(4)]
@@ -141,8 +149,8 @@ def tile_bottleneck_transformer_pb_t_kernel(
             return grouped
 
         def quantise_and_multiply(grouped, s, accs):
-            codes = stage.tile([P, POS], U32, align_bytes=64)
-            scales = stage.tile([P, POS], U8, align_bytes=64)
+            codes = quantised.tile([P, POS], U32, align_bytes=64)
+            scales = quantised.tile([P, POS], U8, align_bytes=64)
             nc.vector.quantize_mx(
                 out=codes[:].bitcast(FP8X4),
                 scales=scales[:],
@@ -187,7 +195,6 @@ def tile_bottleneck_transformer_pb_t_kernel(
                 )
             nc.sync.dma_start(out=out[b].rearrange("(m p) w -> p m w", p=P), in_=rectified[:])
 
-        rows_of = {}
         grouped_of = {}
         accs_of = {}
         chunks = BATCH * PASSES
@@ -196,8 +203,9 @@ def tile_bottleneck_transformer_pb_t_kernel(
             if n < chunks:
                 b, s = divmod(n, PASSES)
                 if s == 0 and b + LOOKAHEAD < BATCH:
-                    rows_of[b + LOOKAHEAD] = load_batch(b + LOOKAHEAD)
-                grouped_of[n] = regroup(rows_of[b][s])
+                    load_h(b + LOOKAHEAD)
+                    load_x(b + LOOKAHEAD)
+                grouped_of[n] = regroup(rows_of[(b, s)])
             if 1 <= n <= chunks:
                 b, s = divmod(n - 1, PASSES)
                 if s == 0:
@@ -210,11 +218,20 @@ def tile_bottleneck_transformer_pb_t_kernel(
                 b = (n - LAG) // PASSES
                 finish_batch(b, accs_of[b][0], accs_of[b][1])
 
-        rows_of[0] = load_batch(0)
+        load_h(0)
+        load_x(0)
+        load_h(1)
         load_weight(conv3_w_words, conv3_w_scales, 0, 1)
+        load_x(1)
+        load_h(2)
+        load_x(2)
         load_weight(sc_w_words, sc_w_scales, 1, 2)
-        for b in range(1, LOOKAHEAD):
-            rows_of[b] = load_batch(b)
+        for b in range(3, LOOKAHEAD):
+            load_h(b)
+            load_x(b)
+
+        cols_ps = psum.tile([P, P], BF16, tag="short1")
+        nc.tensor.transpose(cols_ps[:], bn_rows[:], identity[:])
 
         first_finish = PASSES - 1 + LAG
         for n in range(first_finish):

@@ -27,7 +27,7 @@ EPS = 1e-5
 FLOPS = 2 * BATCH * C_OUT * (C_MAIN + C_SHORT) * POS
 
 VECTOR_COLS = 224
-RUN = 4
+RUN = 8
 LOOKAHEAD = 5
 LAG = 4
 SCALAR_QUEUE_VECTORS = 5

@@ -28,9 +28,10 @@ FLOPS = 2 * BATCH * C_OUT * (C_MAIN + C_SHORT) * POS
 
 VECTOR_COLS = 224
 RUN = 8
+HEAD_BATCHES = 2
 LOOKAHEAD = 5
 LAG = 4
-SCALAR_QUEUE_VECTORS = 5
+SYNC_QUEUE_VECTORS = 5
 
 
 def tile_bottleneck_transformer_pb_t_kernel(
@@ -57,21 +58,27 @@ def tile_bottleneck_transformer_pb_t_kernel(
         ctx.enter_context(tc.manual_schedule())
         const = ctx.enter_context(tc.tile_pool(name="const", bufs=1))
         raw = ctx.enter_context(tc.tile_pool(name="raw", bufs=LOOKAHEAD + 1))
-        stage = ctx.enter_context(tc.tile_pool(name="stage", bufs=3))
+        stage = ctx.enter_context(tc.tile_pool(name="stage", bufs=4))
         quantised = ctx.enter_context(tc.tile_pool(name="quantised", bufs=8))
         result = ctx.enter_context(tc.tile_pool(name="result", bufs=3))
+        stored = ctx.enter_context(tc.tile_pool(name="stored", bufs=6))
         psum = ctx.enter_context(tc.psum_pool(name="psum", bufs=2))
 
         w_words = const.tile([P, PASSES, 2 * C_OUT], U8, align_bytes=64)
         w_scales = const.tile([P, PASSES, C_OUT], U8, align_bytes=64)
+        bn_rows = const.tile([P, P], BF16)
+        nc.vector.memset(bn_rows[:], 0.0)
         nc.vector.memset(w_scales[:].rearrange("p s n -> p (s n)").bitcast(I32), 0)
 
-        def load_weight(words, scales, first_pass, passes):
+        def load_words(words, first_pass, passes):
             mine = slice(first_pass, first_pass + passes)
             nc.sync.dma_start(
                 out=w_words[:, mine, :].bitcast(I32),
                 in_=words.rearrange("g p n -> p g n").bitcast(I32),
             )
+
+        def load_scales(scales, first_pass, passes):
+            mine = slice(first_pass, first_pass + passes)
             for quadrant in range(4):
                 nc.sync.dma_start(
                     out=w_scales[32 * quadrant : 32 * quadrant + 4, mine, :].bitcast(I32),
@@ -89,28 +96,32 @@ def tile_bottleneck_transformer_pb_t_kernel(
 
         def load_x(b):
             x_raw = raw.tile([P, C_SHORT // (P * PACK), PACK, POS], BF16)
-            nc.sync.dma_start(
-                out=x_raw[:], in_=x[b].rearrange("(g p j) w -> p g j w", p=P, j=PACK)
-            )
             rows_of[(b, 1)] = x_raw[:, 0]
             rows_of[(b, 2)] = x_raw[:, 1]
+            rows = x[b].rearrange("(g p j) w -> p g j w", p=P, j=PACK)
+            if b < HEAD_BATCHES:
+                return [
+                    lambda g=g: nc.sync.dma_start(out=x_raw[:, g], in_=rows[:, g])
+                    for g in range(C_SHORT // (P * PACK))
+                ]
+            nc.sync.dma_start(out=x_raw[:], in_=rows)
+            return []
 
-        bn_rows = const.tile([P, P], BF16)
-        nc.vector.memset(bn_rows[:], 0.0)
+        vectors = [bn3_v, scbn_v, bn3_g, scbn_g, bn3_m, scbn_m, bn3_b, scbn_b, sc_b]
+
+        def load_vectors(queue, which):
+            for v in which:
+                queue.dma_start(
+                    out=bn_rows[M_TILES * v : M_TILES * (v + 1), :],
+                    in_=vectors[v].rearrange("(m c) -> m c", m=M_TILES),
+                )
+
+        load_vectors(nc.gpsimd, range(SYNC_QUEUE_VECTORS, len(vectors)))
         identity = const.tile([P, P], BF16)
         make_identity(nc, identity[:])
-        vectors = [bn3_v, scbn_v, bn3_g, scbn_g, bn3_m, scbn_m, bn3_b, scbn_b, sc_b]
-        for v, vector in enumerate(vectors):
-            queue = nc.scalar if v < SCALAR_QUEUE_VECTORS else nc.gpsimd
-            queue.dma_start(
-                out=bn_rows[M_TILES * v : M_TILES * (v + 1), :],
-                in_=vector.rearrange("(m c) -> m c", m=M_TILES),
-            )
 
-        ones = const.tile([P, 1], F32)
-        nc.vector.memset(ones[:], 1.0)
-        warm = const.tile([P, 1], F32)
-        nc.scalar.activation(out=warm[:], in_=ones[:], func=ACT.Sqrt)
+        half = const.tile([P, 4], F32)
+        nc.gpsimd.memset(half[:], -0.5)
 
         scale = const.tile([P, 2 * M_TILES], F32)
         offset = const.tile([P, M_TILES], F32)
@@ -121,20 +132,18 @@ def tile_bottleneck_transformer_pb_t_kernel(
             var, gain, mean, shift = [cols[:, 4 * i : 4 * i + 4] for i in range(4)]
             bias = cols[:, 16:18]
             var_eps = const.tile([P, 4], F32)
-            nc.vector.tensor_scalar_add(out=var_eps[:], in0=var, scalar1=EPS)
-            std = const.tile([P, 4], F32)
-            nc.scalar.activation(out=std[:], in_=var_eps[:], func=ACT.Sqrt)
+            nc.gpsimd.tensor_scalar_add(out=var_eps[:], in0=var, scalar1=EPS)
             rstd = const.tile([P, 4], F32)
-            nc.vector.reciprocal(out=rstd[:], in_=std[:])
-            nc.vector.tensor_mul(out=scale[:], in0=gain, in1=rstd[:])
+            nc.gpsimd.tensor_tensor(out=rstd[:], in0=var_eps[:], in1=half[:], op=ALU.pow)
+            nc.gpsimd.tensor_mul(out=scale[:], in0=gain, in1=rstd[:])
             centre = const.tile([P, 4], F32)
-            nc.vector.tensor_copy(out=centre[:, 0:2], in_=mean[:, 0:2])
-            nc.vector.tensor_sub(out=centre[:, 2:4], in0=mean[:, 2:4], in1=bias)
+            nc.gpsimd.tensor_copy(out=centre[:, 0:2], in_=mean[:, 0:2])
+            nc.gpsimd.tensor_sub(out=centre[:, 2:4], in0=mean[:, 2:4], in1=bias)
             scaled_centre = const.tile([P, 4], F32)
-            nc.vector.tensor_mul(out=scaled_centre[:], in0=centre[:], in1=scale[:])
+            nc.gpsimd.tensor_mul(out=scaled_centre[:], in0=centre[:], in1=scale[:])
             both = const.tile([P, 4], F32)
-            nc.vector.tensor_sub(out=both[:], in0=shift, in1=scaled_centre[:])
-            nc.vector.tensor_add(out=offset[:], in0=both[:, 0:2], in1=both[:, 2:4])
+            nc.gpsimd.tensor_sub(out=both[:], in0=shift, in1=scaled_centre[:])
+            nc.gpsimd.tensor_add(out=offset[:], in0=both[:, 0:2], in1=both[:, 2:4])
 
         def regroup(rows):
             grouped = stage.tile([P, POS, PACK], BF16, align_bytes=64)
@@ -170,7 +179,7 @@ def tile_bottleneck_transformer_pb_t_kernel(
         def finish_batch(b, main, short):
             scaled_main = result.tile([P, M_TILES, POS], F32)
             summed = result.tile([P, M_TILES, POS], F32)
-            rectified = result.tile([P, M_TILES, POS], F32)
+            rectified = stored.tile([P, M_TILES, POS], F32)
             for m in range(M_TILES):
                 nc.scalar.activation(
                     out=scaled_main[:, m, :], in_=main[m][:], func=ACT.Copy, scale=scale[:, m : m + 1]
@@ -219,23 +228,29 @@ def tile_bottleneck_transformer_pb_t_kernel(
                 finish_batch(b, accs_of[b][0], accs_of[b][1])
 
         load_h(0)
-        load_x(0)
+        load_words(conv3_w_words, 0, 1)
+        load_scales(conv3_w_scales, 0, 1)
+        x0_pass1, x0_pass2 = load_x(0)
+        x0_pass1()
+        x0_pass2()
         load_h(1)
-        load_weight(conv3_w_words, conv3_w_scales, 0, 1)
-        load_x(1)
-        load_h(2)
-        load_x(2)
-        load_weight(sc_w_words, sc_w_scales, 1, 2)
-        for b in range(3, LOOKAHEAD):
+        load_words(sc_w_words, 1, 2)
+        load_scales(sc_w_scales, 1, 2)
+        for load in load_x(1):
+            load()
+        load_vectors(nc.sync, range(SYNC_QUEUE_VECTORS))
+        for b in range(2, LOOKAHEAD):
             load_h(b)
-            load_x(b)
-
-        cols_ps = psum.tile([P, P], BF16, tag="short1")
-        nc.tensor.transpose(cols_ps[:], bn_rows[:], identity[:])
+            for load in load_x(b):
+                load()
 
         first_finish = PASSES - 1 + LAG
+        cols_ps = psum.tile([P, P], BF16, tag="short1")
         for n in range(first_finish):
             step(n)
-        fold_batch_norms()
+            if n == PASSES:
+                nc.tensor.transpose(cols_ps[:], bn_rows[:], identity[:])
+            if n == PASSES + 1:
+                fold_batch_norms()
         for n in range(first_finish, chunks + LAG):
             step(n)

@@ -26,11 +26,12 @@ EPS = 1e-5
 
 FLOPS = 2 * BATCH * C_OUT * (C_MAIN + C_SHORT) * POS
 
-VECTOR_COLS = 224
+VECTOR_COLS = 176
+TENSOR_COLS = 256
+TENSOR_FROM = 3
 RUN = 8
 HEAD_BATCHES = 2
 LOOKAHEAD = 5
-LAG = 4
 SYNC_QUEUE_VECTORS = 5
 
 
@@ -62,6 +63,7 @@ def tile_bottleneck_transformer_pb_t_kernel(
         quantised = ctx.enter_context(tc.tile_pool(name="quantised", bufs=8))
         result = ctx.enter_context(tc.tile_pool(name="result", bufs=3))
         stored = ctx.enter_context(tc.tile_pool(name="stored", bufs=6))
+        psum_main = ctx.enter_context(tc.psum_pool(name="psum_main", bufs=1))
         psum = ctx.enter_context(tc.psum_pool(name="psum", bufs=2))
 
         w_words = const.tile([P, PASSES, 2 * C_OUT], U8, align_bytes=64)
@@ -145,12 +147,29 @@ def tile_bottleneck_transformer_pb_t_kernel(
             nc.gpsimd.tensor_sub(out=both[:], in0=shift, in1=scaled_centre[:])
             nc.gpsimd.tensor_add(out=offset[:], in0=both[:, 0:2], in1=both[:, 2:4])
 
-        def regroup(rows):
+        def regroup_on_tensor(rows):
+            regrouped = psum.tile([P, TENSOR_COLS, PACK], BF16)
+            cols = POS // PACK
+            for c in range(0, TENSOR_COLS, cols):
+                first = POS - TENSOR_COLS + c
+                nc.tensor.matmul(
+                    regrouped[:, c : c + cols, :].rearrange("p c j -> p (c j)"),
+                    lhsT=identity[:],
+                    rhs=rows[:, :, first : first + cols].rearrange("p j c -> p c j"),
+                    start=True,
+                    stop=True,
+                )
+            return regrouped
+
+        def regroup(rows, from_tensor):
             grouped = stage.tile([P, POS, PACK], BF16, align_bytes=64)
-            for copy, cols in (
-                (nc.vector.tensor_copy, slice(0, VECTOR_COLS)),
-                (nc.scalar.copy, slice(VECTOR_COLS, POS)),
-            ):
+            split = VECTOR_COLS if from_tensor is None else POS - TENSOR_COLS
+            shares = [(nc.vector.tensor_copy, slice(0, split))]
+            if from_tensor is None:
+                shares.append((nc.scalar.copy, slice(split, POS)))
+            else:
+                nc.scalar.copy(out=grouped[:, split:, :], in_=from_tensor[:])
+            for copy, cols in shares:
                 copy(
                     out=grouped[:, cols, :].rearrange("p (c i) j -> p c j i", i=RUN),
                     in_=rows[:, :, cols].rearrange("p j (c i) -> p c j i", i=RUN),
@@ -176,20 +195,26 @@ def tile_bottleneck_transformer_pb_t_kernel(
                     stop=(s != 1),
                 )
 
-        def finish_batch(b, main, short):
+        def scale_main(b):
             scaled_main = result.tile([P, M_TILES, POS], F32)
+            for m in range(M_TILES):
+                nc.scalar.activation(
+                    out=scaled_main[:, m, :],
+                    in_=main_of[b][m][:],
+                    func=ACT.Copy,
+                    scale=scale[:, m : m + 1],
+                )
+            scaled_of[b] = scaled_main
+
+        def finish_batch(b):
             summed = result.tile([P, M_TILES, POS], F32)
             rectified = stored.tile([P, M_TILES, POS], F32)
             for m in range(M_TILES):
-                nc.scalar.activation(
-                    out=scaled_main[:, m, :], in_=main[m][:], func=ACT.Copy, scale=scale[:, m : m + 1]
-                )
-            for m in range(M_TILES):
                 nc.vector.scalar_tensor_tensor(
                     out=summed[:, m, :],
-                    in0=short[m][:],
+                    in0=short_of[b][m][:],
                     scalar=scale[:, M_TILES + m : M_TILES + m + 1],
-                    in1=scaled_main[:, m, :],
+                    in1=scaled_of[b][:, m, :],
                     op0=ALU.mult,
                     op1=ALU.add,
                 )
@@ -202,30 +227,51 @@ def tile_bottleneck_transformer_pb_t_kernel(
                     op0=ALU.add,
                     op1=ALU.max,
                 )
-            nc.sync.dma_start(out=out[b].rearrange("(m p) w -> p m w", p=P), in_=rectified[:])
+                if b == BATCH - 1:
+                    nc.sync.dma_start(out=out[b, P * m : P * (m + 1), :], in_=rectified[:, m, :])
+            if b < BATCH - 1:
+                nc.sync.dma_start(out=out[b].rearrange("(m p) w -> p m w", p=P), in_=rectified[:])
 
         grouped_of = {}
-        accs_of = {}
+        tensor_of = {}
+        main_of = {}
+        short_of = {}
+        scaled_of = {}
         chunks = BATCH * PASSES
 
         def step(n):
+            b, s = divmod(n, PASSES)
+            if s == PASSES - 1 and TENSOR_FROM <= b + 1 < BATCH:
+                tensor_of[n + 1] = regroup_on_tensor(rows_of[(b + 1, 0)])
             if n < chunks:
-                b, s = divmod(n, PASSES)
                 if s == 0 and b + LOOKAHEAD < BATCH:
                     load_h(b + LOOKAHEAD)
-                    load_x(b + LOOKAHEAD)
-                grouped_of[n] = regroup(rows_of[(b, s)])
+                    for load in load_x(b + LOOKAHEAD):
+                        load()
+                grouped_of[n] = regroup(rows_of[(b, s)], tensor_of.get(n))
+            if s == 2 and 0 < b < BATCH:
+                if b == 1:
+                    scale_main(0)
+                scale_main(b)
             if 1 <= n <= chunks:
-                b, s = divmod(n - 1, PASSES)
-                if s == 0:
-                    accs_of[b] = (
-                        [psum.tile([P, POS], F32, name="main%d" % m) for m in range(M_TILES)],
-                        [psum.tile([P, POS], F32, name="short%d" % m) for m in range(M_TILES)],
-                    )
-                quantise_and_multiply(grouped_of[n - 1], s, accs_of[b][min(s, 1)])
-            if n >= PASSES - 1 + LAG and (n - LAG) % PASSES == PASSES - 1:
-                b = (n - LAG) // PASSES
-                finish_batch(b, accs_of[b][0], accs_of[b][1])
+                b1, s1 = divmod(n - 1, PASSES)
+                if s1 == 0:
+                    main_of[b1] = [
+                        psum.tile([P, POS], F32, name="first%d" % m, tag="regrouped")
+                        if b1 == 0
+                        else psum_main.tile([P, POS], F32, name="main%d" % m)
+                        for m in range(M_TILES)
+                    ]
+                if s1 == 1:
+                    short_of[b1] = [
+                        psum.tile([P, POS], F32, name="short%d" % m) for m in range(M_TILES)
+                    ]
+                accs = main_of[b1] if s1 == 0 else short_of[b1]
+                quantise_and_multiply(grouped_of[n - 1], s1, accs)
+            if n == 6:
+                finish_batch(0)
+            if s == 1 and b >= 2:
+                finish_batch(b - 1)
 
         load_h(0)
         load_words(conv3_w_words, 0, 1)
@@ -233,24 +279,22 @@ def tile_bottleneck_transformer_pb_t_kernel(
         x0_pass1, x0_pass2 = load_x(0)
         x0_pass1()
         x0_pass2()
+        load_vectors(nc.sync, range(SYNC_QUEUE_VECTORS))
         load_h(1)
         load_words(sc_w_words, 1, 2)
+        x1_pass1, x1_pass2 = load_x(1)
+        x1_pass1()
         load_scales(sc_w_scales, 1, 2)
-        for load in load_x(1):
-            load()
-        load_vectors(nc.sync, range(SYNC_QUEUE_VECTORS))
+        x1_pass2()
         for b in range(2, LOOKAHEAD):
             load_h(b)
             for load in load_x(b):
                 load()
 
-        first_finish = PASSES - 1 + LAG
         cols_ps = psum.tile([P, P], BF16, tag="short1")
-        for n in range(first_finish):
+        for n in range(chunks + 2):
             step(n)
-            if n == PASSES:
+            if n == 1:
                 nc.tensor.transpose(cols_ps[:], bn_rows[:], identity[:])
             if n == PASSES + 1:
                 fold_batch_norms()
-        for n in range(first_finish, chunks + LAG):
-            step(n)

@@ -29,6 +29,7 @@ FLOPS = 2 * BATCH * C_OUT * (C_MAIN + C_SHORT) * POS
 VECTOR_COLS = 176
 TENSOR_COLS = 256
 TENSOR_FROM = 3
+GPSIMD_COLS = 160
 RUN = 8
 HEAD_BATCHES = 2
 LOOKAHEAD = 5
@@ -161,20 +162,41 @@ def tile_bottleneck_transformer_pb_t_kernel(
                 )
             return regrouped
 
+        def by_runs(grouped, cols):
+            return grouped[:, cols, :].rearrange("p (c i) j -> p c j i", i=RUN)
+
+        def rows_by_runs(rows, cols):
+            return rows[:, :, cols].rearrange("p j (c i) -> p c j i", i=RUN)
+
         def regroup(rows, from_tensor):
-            grouped = stage.tile([P, POS, PACK], BF16, align_bytes=64)
-            split = VECTOR_COLS if from_tensor is None else POS - TENSOR_COLS
-            shares = [(nc.vector.tensor_copy, slice(0, split))]
             if from_tensor is None:
-                shares.append((nc.scalar.copy, slice(split, POS)))
+                grouped = stage.tile([P, POS, PACK], BF16, align_bytes=64)
+                shares = [
+                    (nc.vector.tensor_copy, slice(0, VECTOR_COLS)),
+                    (nc.scalar.copy, slice(VECTOR_COLS, POS)),
+                ]
             else:
-                nc.scalar.copy(out=grouped[:, split:, :], in_=from_tensor[:])
+                grouped = early_of.pop()
+                shares = [(nc.vector.tensor_copy, slice(GPSIMD_COLS, POS - TENSOR_COLS))]
+                nc.scalar.copy(out=grouped[:, POS - TENSOR_COLS :, :], in_=from_tensor[:])
             for copy, cols in shares:
-                copy(
-                    out=grouped[:, cols, :].rearrange("p (c i) j -> p c j i", i=RUN),
-                    in_=rows[:, :, cols].rearrange("p j (c i) -> p c j i", i=RUN),
-                )
+                copy(out=by_runs(grouped, cols), in_=rows_by_runs(rows, cols))
             return grouped
+
+        early_of = []
+
+        def regroup_on_gpsimd(rows):
+            early = stage.tile([P, POS, PACK], BF16, align_bytes=64, bufs=1)
+            cols = slice(0, GPSIMD_COLS)
+            nc.gpsimd.tensor_scalar(
+                out=by_runs(early, cols),
+                in0=rows_by_runs(rows, cols),
+                scalar1=1.0,
+                scalar2=0.0,
+                op0=ALU.mult,
+                op1=ALU.add,
+            )
+            early_of.append(early)
 
         def quantise_and_multiply(grouped, s, accs):
             codes = quantised.tile([P, POS], U32, align_bytes=64)
@@ -268,6 +290,8 @@ def tile_bottleneck_transformer_pb_t_kernel(
                     ]
                 accs = main_of[b1] if s1 == 0 else short_of[b1]
                 quantise_and_multiply(grouped_of[n - 1], s1, accs)
+            if s == 1 and TENSOR_FROM <= b + 1 < BATCH:
+                regroup_on_gpsimd(rows_of[(b + 1, 0)])
             if n == 6:
                 finish_batch(0)
             if s == 1 and b >= 2:

@@ -26,10 +26,13 @@ EPS = 1e-5
 
 FLOPS = 2 * BATCH * C_OUT * (C_MAIN + C_SHORT) * POS
 
-VECTOR_COLS = 176
-TENSOR_COLS = 256
+HEAD_SHARES = (0, 240, 272, 0)
+SHARES = (
+    (160, 96, 0, 256),
+    (0, 160, 224, 128),
+    (0, 192, 320, 0),
+)
 TENSOR_FROM = 3
-GPSIMD_COLS = 160
 RUN = 8
 HEAD_BATCHES = 2
 LOOKAHEAD = 5
@@ -90,6 +93,11 @@ def tile_bottleneck_transformer_pb_t_kernel(
                     .bitcast(I32),
                 )
 
+        grouped_of = {}
+        regrouped_of = {}
+        main_of = {}
+        short_of = {}
+        scaled_of = {}
         rows_of = {}
 
         def load_h(b):
@@ -148,55 +156,60 @@ def tile_bottleneck_transformer_pb_t_kernel(
             nc.gpsimd.tensor_sub(out=both[:], in0=shift, in1=scaled_centre[:])
             nc.gpsimd.tensor_add(out=offset[:], in0=both[:, 0:2], in1=both[:, 2:4])
 
-        def regroup_on_tensor(rows):
-            regrouped = psum.tile([P, TENSOR_COLS, PACK], BF16)
-            cols = POS // PACK
-            for c in range(0, TENSOR_COLS, cols):
-                first = POS - TENSOR_COLS + c
-                nc.tensor.matmul(
-                    regrouped[:, c : c + cols, :].rearrange("p c j -> p (c j)"),
-                    lhsT=identity[:],
-                    rhs=rows[:, :, first : first + cols].rearrange("p j c -> p c j"),
-                    start=True,
-                    stop=True,
-                )
-            return regrouped
+        def columns_of(b, s):
+            widths = SHARES[s] if b >= TENSOR_FROM else HEAD_SHARES
+            if b == TENSOR_FROM and s == 1:
+                widths = SHARES[2]
+            ends = [sum(widths[: i + 1]) for i in range(len(widths))]
+            return [slice(end - width, end) for width, end in zip(widths, ends)]
 
         def by_runs(grouped, cols):
             return grouped[:, cols, :].rearrange("p (c i) j -> p c j i", i=RUN)
 
-        def rows_by_runs(rows, cols):
-            return rows[:, :, cols].rearrange("p j (c i) -> p c j i", i=RUN)
+        def rows_by_runs(b, s, cols):
+            return rows_of[(b, s)][:, :, cols].rearrange("p j (c i) -> p c j i", i=RUN)
 
-        def regroup(rows, from_tensor):
-            if from_tensor is None:
-                grouped = stage.tile([P, POS, PACK], BF16, align_bytes=64)
-                shares = [
-                    (nc.vector.tensor_copy, slice(0, VECTOR_COLS)),
-                    (nc.scalar.copy, slice(VECTOR_COLS, POS)),
-                ]
-            else:
-                grouped = early_of.pop()
-                shares = [(nc.vector.tensor_copy, slice(GPSIMD_COLS, POS - TENSOR_COLS))]
-                nc.scalar.copy(out=grouped[:, POS - TENSOR_COLS :, :], in_=from_tensor[:])
-            for copy, cols in shares:
-                copy(out=by_runs(grouped, cols), in_=rows_by_runs(rows, cols))
-            return grouped
+        def regroup_on_tensor(b, s):
+            cols = columns_of(b, s)[3]
+            if cols.start < cols.stop:
+                width = cols.stop - cols.start
+                regrouped = psum.tile([P, width, PACK], BF16)
+                part = POS // PACK
+                for c in range(0, width, part):
+                    first = cols.start + c
+                    nc.tensor.matmul(
+                        regrouped[:, c : c + part, :].rearrange("p c j -> p (c j)"),
+                        lhsT=identity[:],
+                        rhs=rows_of[(b, s)][:, :, first : first + part].rearrange("p j c -> p c j"),
+                        start=True,
+                        stop=True,
+                    )
+                regrouped_of[(b, s)] = regrouped
 
-        early_of = []
-
-        def regroup_on_gpsimd(rows):
+        def regroup_on_gpsimd(b, s):
             early = stage.tile([P, POS, PACK], BF16, align_bytes=64, bufs=1)
-            cols = slice(0, GPSIMD_COLS)
+            cols = columns_of(b, s)[0]
             nc.gpsimd.tensor_scalar(
                 out=by_runs(early, cols),
-                in0=rows_by_runs(rows, cols),
+                in0=rows_by_runs(b, s, cols),
                 scalar1=1.0,
                 scalar2=0.0,
                 op0=ALU.mult,
                 op1=ALU.add,
             )
-            early_of.append(early)
+            grouped_of[(b, s)] = early
+
+        def regroup(b, s):
+            if (b, s) not in grouped_of:
+                grouped = stage.tile([P, POS, PACK], BF16, align_bytes=64)
+                grouped_of[(b, s)] = grouped
+            grouped = grouped_of[(b, s)]
+            for_gpsimd, for_vector, for_scalar, for_tensor = columns_of(b, s)
+            if (b, s) in regrouped_of:
+                nc.scalar.copy(out=grouped[:, for_tensor, :], in_=regrouped_of[(b, s)][:])
+            for copy, cols in ((nc.vector.tensor_copy, for_vector), (nc.scalar.copy, for_scalar)):
+                if cols.start < cols.stop:
+                    copy(out=by_runs(grouped, cols), in_=rows_by_runs(b, s, cols))
 
         def quantise_and_multiply(grouped, s, accs):
             codes = quantised.tile([P, POS], U32, align_bytes=64)
@@ -254,23 +267,18 @@ def tile_bottleneck_transformer_pb_t_kernel(
             if b < BATCH - 1:
                 nc.sync.dma_start(out=out[b].rearrange("(m p) w -> p m w", p=P), in_=rectified[:])
 
-        grouped_of = {}
-        tensor_of = {}
-        main_of = {}
-        short_of = {}
-        scaled_of = {}
         chunks = BATCH * PASSES
 
         def step(n):
             b, s = divmod(n, PASSES)
-            if s == PASSES - 1 and TENSOR_FROM <= b + 1 < BATCH:
-                tensor_of[n + 1] = regroup_on_tensor(rows_of[(b + 1, 0)])
+            if n + 1 < chunks:
+                regroup_on_tensor(*divmod(n + 1, PASSES))
             if n < chunks:
                 if s == 0 and b + LOOKAHEAD < BATCH:
                     load_h(b + LOOKAHEAD)
                     for load in load_x(b + LOOKAHEAD):
                         load()
-                grouped_of[n] = regroup(rows_of[(b, s)], tensor_of.get(n))
+                regroup(b, s)
             if s == 2 and 0 < b < BATCH:
                 if b == 1:
                     scale_main(0)
@@ -289,9 +297,9 @@ def tile_bottleneck_transformer_pb_t_kernel(
                         psum.tile([P, POS], F32, name="short%d" % m) for m in range(M_TILES)
                     ]
                 accs = main_of[b1] if s1 == 0 else short_of[b1]
-                quantise_and_multiply(grouped_of[n - 1], s1, accs)
+                quantise_and_multiply(grouped_of[(b1, s1)], s1, accs)
             if s == 1 and TENSOR_FROM <= b + 1 < BATCH:
-                regroup_on_gpsimd(rows_of[(b + 1, 0)])
+                regroup_on_gpsimd(b + 1, 0)
             if n == 6:
                 finish_batch(0)
             if s == 1 and b >= 2:

@@ -178,9 +178,9 @@ def tile_bottleneck_transformer_pb_t_kernel(
                 for c in range(0, width, part):
                     first = cols.start + c
                     nc.tensor.matmul(
-                        regrouped[:, c : c + part, :].rearrange("p c j -> p (c j)"),
+                        regrouped[:, c : c + part, :].rearrange("p c j -> p j c"),
                         lhsT=identity[:],
-                        rhs=rows_of[(b, s)][:, :, first : first + part].rearrange("p j c -> p c j"),
+                        rhs=rows_of[(b, s)][:, :, first : first + part],
                         start=True,
                         stop=True,
                     )

@@ -26,11 +26,11 @@ EPS = 1e-5
 
 FLOPS = 2 * BATCH * C_OUT * (C_MAIN + C_SHORT) * POS
 
-HEAD_SHARES = (0, 240, 272, 0)
+HEAD_SHARES = (0, 208, 304, 0)
 SHARES = (
     (160, 96, 0, 256),
-    (0, 160, 224, 128),
-    (0, 192, 320, 0),
+    (0, 176, 336, 0),
+    (0, 176, 208, 128),
 )
 TENSOR_FROM = 3
 RUN = 8
@@ -158,8 +158,8 @@ def tile_bottleneck_transformer_pb_t_kernel(
 
         def columns_of(b, s):
             widths = SHARES[s] if b >= TENSOR_FROM else HEAD_SHARES
-            if b == TENSOR_FROM and s == 1:
-                widths = SHARES[2]
+            if b == TENSOR_FROM and s == 2:
+                widths = SHARES[1]
             ends = [sum(widths[: i + 1]) for i in range(len(widths))]
             return [slice(end - width, end) for width, end in zip(widths, ends)]
 
@@ -271,8 +271,6 @@ def tile_bottleneck_transformer_pb_t_kernel(
 
         def step(n):
             b, s = divmod(n, PASSES)
-            if n + 1 < chunks:
-                regroup_on_tensor(*divmod(n + 1, PASSES))
             if n < chunks:
                 if s == 0 and b + LOOKAHEAD < BATCH:
                     load_h(b + LOOKAHEAD)
@@ -298,6 +296,8 @@ def tile_bottleneck_transformer_pb_t_kernel(
                     ]
                 accs = main_of[b1] if s1 == 0 else short_of[b1]
                 quantise_and_multiply(grouped_of[(b1, s1)], s1, accs)
+            if n + 2 < chunks:
+                regroup_on_tensor(*divmod(n + 2, PASSES))
             if s == 1 and TENSOR_FROM <= b + 1 < BATCH:
                 regroup_on_gpsimd(b + 1, 0)
             if n == 6:

@@ -29,8 +29,8 @@ FLOPS = 2 * BATCH * C_OUT * (C_MAIN + C_SHORT) * POS
 HEAD_SHARES = (0, 208, 304, 0)
 SHARES = (
     (160, 96, 0, 256),
-    (0, 176, 336, 0),
-    (0, 176, 208, 128),
+    (0, 192, 320, 0),
+    (0, 192, 320, 0),
 )
 TENSOR_FROM = 3
 RUN = 8
@@ -127,9 +127,9 @@ def tile_bottleneck_transformer_pb_t_kernel(
                     in_=vectors[v].rearrange("(m c) -> m c", m=M_TILES),
                 )
 
-        load_vectors(nc.gpsimd, range(SYNC_QUEUE_VECTORS, len(vectors)))
         identity = const.tile([P, P], BF16)
         make_identity(nc, identity[:])
+        load_vectors(nc.gpsimd, range(SYNC_QUEUE_VECTORS, len(vectors)))
 
         half = const.tile([P, 4], F32)
         nc.gpsimd.memset(half[:], -0.5)
@@ -158,8 +158,6 @@ def tile_bottleneck_transformer_pb_t_kernel(
 
         def columns_of(b, s):
             widths = SHARES[s] if b >= TENSOR_FROM else HEAD_SHARES
-            if b == TENSOR_FROM and s == 2:
-                widths = SHARES[1]
             ends = [sum(widths[: i + 1]) for i in range(len(widths))]
             return [slice(end - width, end) for width, end in zip(widths, ends)]
 

@@ -29,10 +29,11 @@ FLOPS = 2 * BATCH * C_OUT * (C_MAIN + C_SHORT) * POS
 HEAD_SHARES = (0, 208, 304, 0)
 SHARES = (
     (160, 96, 0, 256),
-    (0, 192, 320, 0),
-    (0, 192, 320, 0),
+    (0, 160, 352, 0),
+    (0, 160, 352, 0),
 )
-TENSOR_FROM = 3
+TENSOR_FROM = 2
+GPSIMD_FROM = 3
 RUN = 8
 HEAD_BATCHES = 2
 LOOKAHEAD = 5
@@ -98,6 +99,7 @@ def tile_bottleneck_transformer_pb_t_kernel(
         main_of = {}
         short_of = {}
         scaled_of = {}
+        summed_of = {}
         rows_of = {}
 
         def load_h(b):
@@ -158,6 +160,8 @@ def tile_bottleneck_transformer_pb_t_kernel(
 
         def columns_of(b, s):
             widths = SHARES[s] if b >= TENSOR_FROM else HEAD_SHARES
+            if b == 2 and s == 0:
+                widths = (0, 208, 48, 256)
             ends = [sum(widths[: i + 1]) for i in range(len(widths))]
             return [slice(end - width, end) for width, end in zip(widths, ends)]
 
@@ -188,8 +192,8 @@ def tile_bottleneck_transformer_pb_t_kernel(
             early = stage.tile([P, POS, PACK], BF16, align_bytes=64, bufs=1)
             cols = columns_of(b, s)[0]
             nc.gpsimd.tensor_scalar(
-                out=by_runs(early, cols),
-                in0=rows_by_runs(b, s, cols),
+                out=early[:, cols, :],
+                in0=rows_of[(b, s)][:, :, cols].rearrange("p j c -> p c j"),
                 scalar1=1.0,
                 scalar2=0.0,
                 op0=ALU.mult,
@@ -239,9 +243,8 @@ def tile_bottleneck_transformer_pb_t_kernel(
                 )
             scaled_of[b] = scaled_main
 
-        def finish_batch(b):
+        def add_short(b):
             summed = result.tile([P, M_TILES, POS], F32)
-            rectified = stored.tile([P, M_TILES, POS], F32)
             for m in range(M_TILES):
                 nc.vector.scalar_tensor_tensor(
                     out=summed[:, m, :],
@@ -251,15 +254,27 @@ def tile_bottleneck_transformer_pb_t_kernel(
                     op0=ALU.mult,
                     op1=ALU.add,
                 )
+            summed_of[b] = summed
+
+        def rectify(b):
+            rectified = stored.tile([P, M_TILES, POS], F32)
             for m in range(M_TILES):
-                nc.vector.tensor_scalar(
-                    out=rectified[:, m, :],
-                    in0=summed[:, m, :],
-                    scalar1=offset[:, m : m + 1],
-                    scalar2=0.0,
-                    op0=ALU.add,
-                    op1=ALU.max,
-                )
+                if b == BATCH - 1 and m == 0:
+                    nc.scalar.activation(
+                        out=rectified[:, m, :],
+                        in_=summed_of[b][:, m, :],
+                        func=ACT.Relu,
+                        bias=offset[:, m : m + 1],
+                    )
+                else:
+                    nc.vector.tensor_scalar(
+                        out=rectified[:, m, :],
+                        in0=summed_of[b][:, m, :],
+                        scalar1=offset[:, m : m + 1],
+                        scalar2=0.0,
+                        op0=ALU.add,
+                        op1=ALU.max,
+                    )
                 if b == BATCH - 1:
                     nc.sync.dma_start(out=out[b, P * m : P * (m + 1), :], in_=rectified[:, m, :])
             if b < BATCH - 1:
@@ -283,7 +298,7 @@ def tile_bottleneck_transformer_pb_t_kernel(
                 b1, s1 = divmod(n - 1, PASSES)
                 if s1 == 0:
                     main_of[b1] = [
-                        psum.tile([P, POS], F32, name="first%d" % m, tag="regrouped")
+                        psum.tile([P, POS], F32, name="first%d" % m, tag="short%d" % m)
                         if b1 == 0
                         else psum_main.tile([P, POS], F32, name="main%d" % m)
                         for m in range(M_TILES)
@@ -296,12 +311,17 @@ def tile_bottleneck_transformer_pb_t_kernel(
                 quantise_and_multiply(grouped_of[(b1, s1)], s1, accs)
             if n + 2 < chunks:
                 regroup_on_tensor(*divmod(n + 2, PASSES))
-            if s == 1 and TENSOR_FROM <= b + 1 < BATCH:
+            if s == 1 and GPSIMD_FROM <= b + 1 < BATCH:
                 regroup_on_gpsimd(b + 1, 0)
             if n == 6:
-                finish_batch(0)
+                add_short(0)
+                rectify(0)
             if s == 1 and b >= 2:
-                finish_batch(b - 1)
+                add_short(b - 1)
+                if b != BATCH - 1:
+                    rectify(b - 1)
+            if n == chunks:
+                rectify(BATCH - 2)
 
         load_h(0)
         load_words(conv3_w_words, 0, 1)
@@ -321,7 +341,7 @@ def tile_bottleneck_transformer_pb_t_kernel(
             for load in load_x(b):
                 load()
 
-        cols_ps = psum.tile([P, P], BF16, tag="short1")
+        cols_ps = psum.tile([P, P], BF16, tag="regrouped")
         for n in range(chunks + 2):
             step(n)
             if n == 1:

@@ -26,18 +26,17 @@ EPS = 1e-5
 
 FLOPS = 2 * BATCH * C_OUT * (C_MAIN + C_SHORT) * POS
 
-HEAD_SHARES = (0, 208, 304, 0)
+HEAD_SHARES = (0, 224, 288, 0)
 SHARES = (
     (160, 96, 0, 256),
-    (0, 160, 352, 0),
-    (0, 160, 352, 0),
+    (0, 176, 336, 0),
+    (0, 192, 320, 0),
 )
 TENSOR_FROM = 2
 GPSIMD_FROM = 3
 RUN = 8
 HEAD_BATCHES = 2
-LOOKAHEAD = 5
-SYNC_QUEUE_VECTORS = 5
+LOOKAHEAD = 6
 
 
 def tile_bottleneck_transformer_pb_t_kernel(
@@ -67,14 +66,16 @@ def tile_bottleneck_transformer_pb_t_kernel(
         stage = ctx.enter_context(tc.tile_pool(name="stage", bufs=4))
         quantised = ctx.enter_context(tc.tile_pool(name="quantised", bufs=8))
         result = ctx.enter_context(tc.tile_pool(name="result", bufs=3))
-        stored = ctx.enter_context(tc.tile_pool(name="stored", bufs=6))
+        stored = ctx.enter_context(tc.tile_pool(name="stored", bufs=12))
         psum_main = ctx.enter_context(tc.psum_pool(name="psum_main", bufs=1))
         psum = ctx.enter_context(tc.psum_pool(name="psum", bufs=2))
 
         w_words = const.tile([P, PASSES, 2 * C_OUT], U8, align_bytes=64)
         w_scales = const.tile([P, PASSES, C_OUT], U8, align_bytes=64)
-        bn_rows = const.tile([P, P], BF16)
-        nc.vector.memset(bn_rows[:], 0.0)
+        scale_rows = const.tile([P, P], BF16)
+        nc.vector.memset(scale_rows[:], 0.0)
+        offset_rows = const.tile([P, P], BF16)
+        nc.vector.memset(offset_rows[:], 0.0)
         nc.vector.memset(w_scales[:].rearrange("p s n -> p (s n)").bitcast(I32), 0)
 
         def load_words(words, first_pass, passes):
@@ -120,35 +121,45 @@ def tile_bottleneck_transformer_pb_t_kernel(
             nc.sync.dma_start(out=x_raw[:], in_=rows)
             return []
 
-        vectors = [bn3_v, scbn_v, bn3_g, scbn_g, bn3_m, scbn_m, bn3_b, scbn_b, sc_b]
+        scale_vectors = [bn3_v, scbn_v, bn3_g, scbn_g]
+        offset_vectors = [bn3_m, scbn_m, bn3_b, scbn_b, sc_b]
 
-        def load_vectors(queue, which):
-            for v in which:
+        def load_vectors(queue, rows, vectors):
+            for v, vector in enumerate(vectors):
                 queue.dma_start(
-                    out=bn_rows[M_TILES * v : M_TILES * (v + 1), :],
-                    in_=vectors[v].rearrange("(m c) -> m c", m=M_TILES),
+                    out=rows[M_TILES * v : M_TILES * (v + 1), :],
+                    in_=vector.rearrange("(m c) -> m c", m=M_TILES),
                 )
 
         identity = const.tile([P, P], BF16)
         make_identity(nc, identity[:])
-        load_vectors(nc.gpsimd, range(SYNC_QUEUE_VECTORS, len(vectors)))
+        load_vectors(nc.gpsimd, offset_rows, offset_vectors)
 
-        half = const.tile([P, 4], F32)
-        nc.gpsimd.memset(half[:], -0.5)
+        ones = const.tile([P, 1], F32)
+        nc.vector.memset(ones[:], 1.0)
+        warm = const.tile([P, 1], F32)
+        nc.scalar.activation(out=warm[:], in_=ones[:], func=ACT.Sqrt)
 
         scale = const.tile([P, 2 * M_TILES], F32)
         offset = const.tile([P, M_TILES], F32)
+        gains = const.tile([P, 8], F32)
+        std = const.tile([P, 4], F32)
+        rstd = const.tile([P, 4], F32)
 
-        def fold_batch_norms():
-            cols = const.tile([P, M_TILES * len(vectors)], F32)
-            nc.vector.tensor_copy(out=cols[:], in_=cols_ps[:, 0 : M_TILES * len(vectors)])
-            var, gain, mean, shift = [cols[:, 4 * i : 4 * i + 4] for i in range(4)]
-            bias = cols[:, 16:18]
+        def fold_variances():
+            nc.vector.tensor_copy(out=gains[:], in_=cols_ps[:, 0:8])
             var_eps = const.tile([P, 4], F32)
-            nc.gpsimd.tensor_scalar_add(out=var_eps[:], in0=var, scalar1=EPS)
-            rstd = const.tile([P, 4], F32)
-            nc.gpsimd.tensor_tensor(out=rstd[:], in0=var_eps[:], in1=half[:], op=ALU.pow)
-            nc.gpsimd.tensor_mul(out=scale[:], in0=gain, in1=rstd[:])
+            nc.vector.tensor_scalar_add(out=var_eps[:], in0=gains[:, 0:4], scalar1=EPS)
+            nc.scalar.activation(out=std[:], in_=var_eps[:], func=ACT.Sqrt)
+
+        def fold_scales():
+            nc.vector.reciprocal(out=rstd[:], in_=std[:])
+            nc.vector.tensor_mul(out=scale[:], in0=gains[:, 4:8], in1=rstd[:])
+
+        def fold_offsets():
+            shifts = const.tile([P, 10], F32)
+            nc.vector.tensor_copy(out=shifts[:], in_=cols_ps[:, P : P + 10])
+            mean, shift, bias = shifts[:, 0:4], shifts[:, 4:8], shifts[:, 8:10]
             centre = const.tile([P, 4], F32)
             nc.gpsimd.tensor_copy(out=centre[:, 0:2], in_=mean[:, 0:2])
             nc.gpsimd.tensor_sub(out=centre[:, 2:4], in0=mean[:, 2:4], in1=bias)
@@ -315,10 +326,12 @@ def tile_bottleneck_transformer_pb_t_kernel(
                 regroup_on_gpsimd(b + 1, 0)
             if n == 6:
                 add_short(0)
+            if n == 8:
                 rectify(0)
+                rectify(1)
             if s == 1 and b >= 2:
                 add_short(b - 1)
-                if b != BATCH - 1:
+                if b > 2 and b != BATCH - 1:
                     rectify(b - 1)
             if n == chunks:
                 rectify(BATCH - 2)
@@ -329,7 +342,7 @@ def tile_bottleneck_transformer_pb_t_kernel(
         x0_pass1, x0_pass2 = load_x(0)
         x0_pass1()
         x0_pass2()
-        load_vectors(nc.sync, range(SYNC_QUEUE_VECTORS))
+        load_vectors(nc.sync, scale_rows, scale_vectors)
         load_h(1)
         load_words(sc_w_words, 1, 2)
         x1_pass1, x1_pass2 = load_x(1)
@@ -341,10 +354,16 @@ def tile_bottleneck_transformer_pb_t_kernel(
             for load in load_x(b):
                 load()
 
-        cols_ps = psum.tile([P, P], BF16, tag="regrouped")
+        cols_ps = psum.tile([P, 2 * P], BF16, tag="regrouped")
         for n in range(chunks + 2):
             step(n)
             if n == 1:
-                nc.tensor.transpose(cols_ps[:], bn_rows[:], identity[:])
-            if n == PASSES + 1:
-                fold_batch_norms()
+                nc.tensor.transpose(cols_ps[:, 0:P], scale_rows[:], identity[:])
+            if n == 3:
+                fold_variances()
+            if n == 4:
+                fold_scales()
+            if n == 5:
+                nc.tensor.transpose(cols_ps[:, P : 2 * P], offset_rows[:], identity[:])
+            if n == 6:
+                fold_offsets()

@@ -21,21 +21,20 @@ C_SHORT = 1024
 C_OUT = 256
 M_TILES = C_OUT // P
 POS = 512
-PASSES = (C_MAIN + C_SHORT) // (P * PACK)
+X_PASSES = C_SHORT // (P * PACK)
+PASSES = 1 + X_PASSES
 EPS = 1e-5
 
 FLOPS = 2 * BATCH * C_OUT * (C_MAIN + C_SHORT) * POS
 
-HEAD_SHARES = (0, 224, 288, 0)
-SHARES = (
-    (160, 96, 0, 256),
-    (0, 176, 336, 0),
-    (0, 192, 320, 0),
-)
-TENSOR_FROM = 2
-GPSIMD_FROM = 3
 RUN = 8
 HEAD_BATCHES = 2
+HEAD_SCALAR = 304
+H2_SCALAR = 48
+H2_VECTOR = 208
+X_SCALAR = 296
+H_GPSIMD = 160
+BANK_COLS = 256
 LOOKAHEAD = 6
 
 
@@ -63,9 +62,9 @@ def tile_bottleneck_transformer_pb_t_kernel(
         ctx.enter_context(tc.manual_schedule())
         const = ctx.enter_context(tc.tile_pool(name="const", bufs=1))
         raw = ctx.enter_context(tc.tile_pool(name="raw", bufs=LOOKAHEAD + 1))
-        stage = ctx.enter_context(tc.tile_pool(name="stage", bufs=4))
-        quantised = ctx.enter_context(tc.tile_pool(name="quantised", bufs=8))
-        result = ctx.enter_context(tc.tile_pool(name="result", bufs=3))
+        stage = ctx.enter_context(tc.tile_pool(name="stage", bufs=3))
+        quantised = ctx.enter_context(tc.tile_pool(name="quantised", bufs=3))
+        result = ctx.enter_context(tc.tile_pool(name="result", bufs=2))
         stored = ctx.enter_context(tc.tile_pool(name="stored", bufs=12))
         psum_main = ctx.enter_context(tc.psum_pool(name="psum_main", bufs=1))
         psum = ctx.enter_context(tc.psum_pool(name="psum", bufs=2))
@@ -95,28 +94,29 @@ def tile_bottleneck_transformer_pb_t_kernel(
                     .bitcast(I32),
                 )
 
-        grouped_of = {}
-        regrouped_of = {}
+        h_rows = {}
+        x_rows = {}
+        h_grouped = {}
+        x_grouped = {}
+        h_banks = {}
         main_of = {}
         short_of = {}
         scaled_of = {}
         summed_of = {}
-        rows_of = {}
 
         def load_h(b):
             h_raw = raw.tile([P, PACK, POS], BF16)
             nc.sync.dma_start(out=h_raw[:], in_=h_attn[b].rearrange("(p j) w -> p j w", j=PACK))
-            rows_of[(b, 0)] = h_raw[:]
+            h_rows[b] = h_raw
 
         def load_x(b):
-            x_raw = raw.tile([P, C_SHORT // (P * PACK), PACK, POS], BF16)
-            rows_of[(b, 1)] = x_raw[:, 0]
-            rows_of[(b, 2)] = x_raw[:, 1]
+            x_raw = raw.tile([P, X_PASSES, PACK, POS], BF16)
+            x_rows[b] = x_raw
             rows = x[b].rearrange("(g p j) w -> p g j w", p=P, j=PACK)
             if b < HEAD_BATCHES:
                 return [
                     lambda g=g: nc.sync.dma_start(out=x_raw[:, g], in_=rows[:, g])
-                    for g in range(C_SHORT // (P * PACK))
+                    for g in range(X_PASSES)
                 ]
             nc.sync.dma_start(out=x_raw[:], in_=rows)
             return []
@@ -169,89 +169,136 @@ def tile_bottleneck_transformer_pb_t_kernel(
             nc.gpsimd.tensor_sub(out=both[:], in0=shift, in1=scaled_centre[:])
             nc.gpsimd.tensor_add(out=offset[:], in0=both[:, 0:2], in1=both[:, 2:4])
 
-        def columns_of(b, s):
-            widths = SHARES[s] if b >= TENSOR_FROM else HEAD_SHARES
-            if b == 2 and s == 0:
-                widths = (0, 208, 48, 256)
-            ends = [sum(widths[: i + 1]) for i in range(len(widths))]
-            return [slice(end - width, end) for width, end in zip(widths, ends)]
+        def interleave(copy, grouped, rows, cols):
+            if len(rows.shape) == 4:
+                copy(
+                    out=grouped[:, :, cols, :].rearrange("p g (c i) j -> p g c j i", i=RUN),
+                    in_=rows[:, :, :, cols].rearrange("p g j (c i) -> p g c j i", i=RUN),
+                )
+            else:
+                copy(
+                    out=grouped[:, cols, :].rearrange("p (c i) j -> p c j i", i=RUN),
+                    in_=rows[:, :, cols].rearrange("p j (c i) -> p c j i", i=RUN),
+                )
 
-        def by_runs(grouped, cols):
-            return grouped[:, cols, :].rearrange("p (c i) j -> p c j i", i=RUN)
-
-        def rows_by_runs(b, s, cols):
-            return rows_of[(b, s)][:, :, cols].rearrange("p j (c i) -> p c j i", i=RUN)
-
-        def regroup_on_tensor(b, s):
-            cols = columns_of(b, s)[3]
-            if cols.start < cols.stop:
-                width = cols.stop - cols.start
-                regrouped = psum.tile([P, width, PACK], BF16)
-                part = POS // PACK
-                for c in range(0, width, part):
-                    first = cols.start + c
+        def regroup_h_on_tensor(b, first):
+            h_banks[b] = []
+            part = POS // PACK
+            for start in range(first, POS, BANK_COLS):
+                stop = min(start + BANK_COLS, POS)
+                regrouped = psum.tile([P, stop - start, PACK], BF16)
+                for c in range(start, stop, part):
+                    end = min(c + part, stop)
                     nc.tensor.matmul(
-                        regrouped[:, c : c + part, :].rearrange("p c j -> p j c"),
+                        regrouped[:, c - start : end - start, :].rearrange("p c j -> p j c"),
                         lhsT=identity[:],
-                        rhs=rows_of[(b, s)][:, :, first : first + part],
+                        rhs=h_rows[b][:, :, c:end],
                         start=True,
                         stop=True,
                     )
-                regrouped_of[(b, s)] = regrouped
+                h_banks[b].append((slice(start, stop), regrouped))
 
-        def regroup_on_gpsimd(b, s):
+        def copy_h_banks(b):
+            for cols, regrouped in h_banks[b]:
+                nc.scalar.copy(out=h_grouped[b][:, cols, :], in_=regrouped[:])
+
+        def regroup_h_on_gpsimd(b):
             early = stage.tile([P, POS, PACK], BF16, align_bytes=64, bufs=1)
-            cols = columns_of(b, s)[0]
+            cols = slice(0, H_GPSIMD)
             nc.gpsimd.tensor_scalar(
                 out=early[:, cols, :],
-                in0=rows_of[(b, s)][:, :, cols].rearrange("p j c -> p c j"),
+                in0=h_rows[b][:, :, cols].rearrange("p j c -> p c j"),
                 scalar1=1.0,
                 scalar2=0.0,
                 op0=ALU.mult,
                 op1=ALU.add,
             )
-            grouped_of[(b, s)] = early
+            h_grouped[b] = early
 
-        def regroup(b, s):
-            if (b, s) not in grouped_of:
-                grouped = stage.tile([P, POS, PACK], BF16, align_bytes=64)
-                grouped_of[(b, s)] = grouped
-            grouped = grouped_of[(b, s)]
-            for_gpsimd, for_vector, for_scalar, for_tensor = columns_of(b, s)
-            if (b, s) in regrouped_of:
-                nc.scalar.copy(out=grouped[:, for_tensor, :], in_=regrouped_of[(b, s)][:])
-            for copy, cols in ((nc.vector.tensor_copy, for_vector), (nc.scalar.copy, for_scalar)):
-                if cols.start < cols.stop:
-                    copy(out=by_runs(grouped, cols), in_=rows_by_runs(b, s, cols))
+        def regroup_head_h(b, scalar_cols, vector_cols):
+            grouped_h = stage.tile([P, POS, PACK], BF16, align_bytes=64)
+            h_grouped[b] = grouped_h
+            interleave(nc.vector.tensor_copy, grouped_h, h_rows[b], vector_cols)
+            interleave(nc.scalar.copy, grouped_h, h_rows[b], scalar_cols)
 
-        def quantise_and_multiply(grouped, s, accs):
-            codes = quantised.tile([P, POS], U32, align_bytes=64)
-            scales = quantised.tile([P, POS], U8, align_bytes=64)
-            nc.vector.quantize_mx(
-                out=codes[:].bitcast(FP8X4),
-                scales=scales[:],
-                in_=grouped[:].rearrange("p w j -> p (w j)"),
-            )
+        def new_x(b):
+            grouped_x = stage.tile([P, X_PASSES, POS, PACK], BF16, align_bytes=64)
+            x_grouped[b] = grouped_x
+
+        def regroup_x_pass(b, g, split):
+            if g == 0:
+                new_x(b)
+            for copy, cols in (
+                (nc.vector.tensor_copy, slice(split, POS)),
+                (nc.scalar.copy, slice(0, split)),
+            ):
+                interleave(copy, x_grouped[b][:, g], x_rows[b][:, g], cols)
+
+        def regroup_x(b):
+            new_x(b)
+            interleave(nc.vector.tensor_copy, x_grouped[b], x_rows[b], slice(X_SCALAR, POS))
+            interleave(nc.scalar.copy, x_grouped[b], x_rows[b], slice(0, X_SCALAR))
+
+        def multiply(s, codes, scales, accs):
             for m in range(M_TILES):
                 nc.tensor.matmul_mx(
                     out=accs[m][:],
                     lhsT=w_words[:, s, 2 * P * m : 2 * P * (m + 1)].bitcast(FP4X4),
                     lhsT_scale=w_scales[:, s, P * m : P * (m + 1)],
-                    rhs=codes[:].bitcast(FP8X4),
-                    rhs_scale=scales[:],
-                    start=(s != 2),
+                    rhs=codes.bitcast(FP8X4),
+                    rhs_scale=scales,
+                    start=(s != PASSES - 1),
                     stop=(s != 1),
                 )
+
+        def quantise_h(b):
+            h_codes = quantised.tile([P, POS], U32, align_bytes=64)
+            h_scales = quantised.tile([P, POS], U8, align_bytes=64)
+            nc.vector.quantize_mx(
+                out=h_codes[:].bitcast(FP8X4),
+                scales=h_scales[:],
+                in_=h_grouped[b][:].rearrange("p w j -> p (w j)"),
+            )
+            main_of[b] = [
+                psum.tile([P, POS], F32, name="first%d" % m, tag="short%d" % m)
+                if b == 0
+                else psum_main.tile([P, POS], F32, name="main%d" % m)
+                for m in range(M_TILES)
+            ]
+            multiply(0, h_codes[:], h_scales[:], main_of[b])
+
+        def quantise_x(b, passes):
+            if passes[0] == 0:
+                short_of[b] = [psum.tile([P, POS], F32, name="short%d" % m) for m in range(M_TILES)]
+            n = len(passes)
+            x_codes = quantised.tile([P, X_PASSES, POS], U32, align_bytes=64)
+            x_scales = quantised.tile([P, X_PASSES, POS], U8, align_bytes=64)
+            nc.vector.quantize_mx(
+                out=x_codes[:, 0:n].rearrange("p g w -> p (g w)").bitcast(FP8X4),
+                scales=x_scales[:, 0:n].rearrange("p g w -> p (g w)"),
+                in_=x_grouped[b][:, passes[0] : passes[0] + n].rearrange("p g w j -> p (g w j)"),
+            )
+            for i, g in enumerate(passes):
+                multiply(1 + g, x_codes[:, i, :], x_scales[:, i, :], short_of[b])
 
         def scale_main(b):
             scaled_main = result.tile([P, M_TILES, POS], F32)
             for m in range(M_TILES):
-                nc.scalar.activation(
-                    out=scaled_main[:, m, :],
-                    in_=main_of[b][m][:],
-                    func=ACT.Copy,
-                    scale=scale[:, m : m + 1],
-                )
+                if b < HEAD_BATCHES:
+                    nc.scalar.activation(
+                        out=scaled_main[:, m, :],
+                        in_=main_of[b][m][:],
+                        func=ACT.Copy,
+                        scale=scale[:, m : m + 1],
+                    )
+                else:
+                    nc.scalar.activation(
+                        out=scaled_main[:, m, :],
+                        in_=main_of[b][m][:],
+                        func=ACT.Identity,
+                        scale=scale[:, m : m + 1],
+                        bias=offset[:, m : m + 1],
+                    )
             scaled_of[b] = scaled_main
 
         def add_short(b):
@@ -269,15 +316,8 @@ def tile_bottleneck_transformer_pb_t_kernel(
 
         def rectify(b):
             rectified = stored.tile([P, M_TILES, POS], F32)
-            for m in range(M_TILES):
-                if b == BATCH - 1 and m == 0:
-                    nc.scalar.activation(
-                        out=rectified[:, m, :],
-                        in_=summed_of[b][:, m, :],
-                        func=ACT.Relu,
-                        bias=offset[:, m : m + 1],
-                    )
-                else:
+            if b < HEAD_BATCHES:
+                for m in range(M_TILES):
                     nc.vector.tensor_scalar(
                         out=rectified[:, m, :],
                         in0=summed_of[b][:, m, :],
@@ -286,55 +326,32 @@ def tile_bottleneck_transformer_pb_t_kernel(
                         op0=ALU.add,
                         op1=ALU.max,
                     )
-                if b == BATCH - 1:
-                    nc.sync.dma_start(out=out[b, P * m : P * (m + 1), :], in_=rectified[:, m, :])
-            if b < BATCH - 1:
-                nc.sync.dma_start(out=out[b].rearrange("(m p) w -> p m w", p=P), in_=rectified[:])
+            else:
+                nc.vector.tensor_scalar_max(
+                    out=rectified[:].rearrange("p m w -> p (m w)"),
+                    in0=summed_of[b][:].rearrange("p m w -> p (m w)"),
+                    scalar1=0.0,
+                )
+            nc.sync.dma_start(out=out[b].rearrange("(m p) w -> p m w", p=P), in_=rectified[:])
 
-        chunks = BATCH * PASSES
+        def rectify_last(b):
+            rectified = stored.tile([P, M_TILES, POS], F32)
+            for m in range(M_TILES):
+                if m == 0:
+                    nc.scalar.activation(
+                        out=rectified[:, m, :], in_=summed_of[b][:, m, :], func=ACT.Relu
+                    )
+                else:
+                    nc.vector.tensor_scalar_max(
+                        out=rectified[:, m, :], in0=summed_of[b][:, m, :], scalar1=0.0
+                    )
+                nc.sync.dma_start(out=out[b, P * m : P * (m + 1), :], in_=rectified[:, m, :])
 
-        def step(n):
-            b, s = divmod(n, PASSES)
-            if n < chunks:
-                if s == 0 and b + LOOKAHEAD < BATCH:
-                    load_h(b + LOOKAHEAD)
-                    for load in load_x(b + LOOKAHEAD):
-                        load()
-                regroup(b, s)
-            if s == 2 and 0 < b < BATCH:
-                if b == 1:
-                    scale_main(0)
-                scale_main(b)
-            if 1 <= n <= chunks:
-                b1, s1 = divmod(n - 1, PASSES)
-                if s1 == 0:
-                    main_of[b1] = [
-                        psum.tile([P, POS], F32, name="first%d" % m, tag="short%d" % m)
-                        if b1 == 0
-                        else psum_main.tile([P, POS], F32, name="main%d" % m)
-                        for m in range(M_TILES)
-                    ]
-                if s1 == 1:
-                    short_of[b1] = [
-                        psum.tile([P, POS], F32, name="short%d" % m) for m in range(M_TILES)
-                    ]
-                accs = main_of[b1] if s1 == 0 else short_of[b1]
-                quantise_and_multiply(grouped_of[(b1, s1)], s1, accs)
-            if n + 2 < chunks:
-                regroup_on_tensor(*divmod(n + 2, PASSES))
-            if s == 1 and GPSIMD_FROM <= b + 1 < BATCH:
-                regroup_on_gpsimd(b + 1, 0)
-            if n == 6:
-                add_short(0)
-            if n == 8:
-                rectify(0)
-                rectify(1)
-            if s == 1 and b >= 2:
-                add_short(b - 1)
-                if b > 2 and b != BATCH - 1:
-                    rectify(b - 1)
-            if n == chunks:
-                rectify(BATCH - 2)
+        def load(b):
+            if b < BATCH:
+                load_h(b)
+                for load_piece in load_x(b):
+                    load_piece()
 
         load_h(0)
         load_words(conv3_w_words, 0, 1)
@@ -355,15 +372,58 @@ def tile_bottleneck_transformer_pb_t_kernel(
                 load()
 
         cols_ps = psum.tile([P, 2 * P], BF16, tag="regrouped")
-        for n in range(chunks + 2):
-            step(n)
-            if n == 1:
-                nc.tensor.transpose(cols_ps[:, 0:P], scale_rows[:], identity[:])
-            if n == 3:
-                fold_variances()
-            if n == 4:
-                fold_scales()
-            if n == 5:
-                nc.tensor.transpose(cols_ps[:, P : 2 * P], offset_rows[:], identity[:])
-            if n == 6:
-                fold_offsets()
+
+        head_split = HEAD_SCALAR
+        scalar_cols, vector_cols = slice(0, head_split), slice(head_split, POS)
+        regroup_head_h(0, scalar_cols, vector_cols)
+        load(LOOKAHEAD)
+        regroup_x_pass(0, 0, head_split)
+        quantise_h(0)
+        nc.tensor.transpose(cols_ps[:, 0:P], scale_rows[:], identity[:])
+        regroup_x_pass(0, 1, head_split)
+        quantise_x(0, [0])
+        regroup_head_h(1, scalar_cols, vector_cols)
+        load(1 + LOOKAHEAD)
+        quantise_x(0, [1])
+        fold_variances()
+        regroup_x_pass(1, 0, head_split)
+        quantise_h(1)
+        regroup_h_on_tensor(2, H2_SCALAR + H2_VECTOR)
+        fold_scales()
+        regroup_x_pass(1, 1, head_split)
+        scale_main(0)
+        scale_main(1)
+        quantise_x(1, [0])
+        nc.tensor.transpose(cols_ps[:, P : 2 * P], offset_rows[:], identity[:])
+        regroup_head_h(2, slice(0, H2_SCALAR), slice(H2_SCALAR, H2_SCALAR + H2_VECTOR))
+        copy_h_banks(2)
+        load(2 + LOOKAHEAD)
+        quantise_x(1, [1])
+        add_short(0)
+        fold_offsets()
+        regroup_x(2)
+        quantise_h(2)
+        regroup_h_on_tensor(3, H_GPSIMD)
+        regroup_h_on_gpsimd(3)
+        add_short(1)
+        rectify(0)
+
+        for b in range(HEAD_BATCHES, BATCH):
+            last = b == BATCH - 1
+            load(b + 1 + LOOKAHEAD)
+            if last:
+                quantise_x(b, [0])
+                quantise_x(b, [1])
+            else:
+                quantise_x(b, [0, 1])
+            rectify(b - 1)
+            scale_main(b)
+            if not last:
+                copy_h_banks(b + 1)
+                regroup_x(b + 1)
+                quantise_h(b + 1)
+            if b + 2 < BATCH:
+                regroup_h_on_tensor(b + 2, H_GPSIMD)
+                regroup_h_on_gpsimd(b + 2)
+            add_short(b)
+        rectify_last(BATCH - 1)

@@ -183,16 +183,14 @@ def tile_bottleneck_transformer_pb_t_kernel(
 
         def regroup_h_on_tensor(b, first):
             h_banks[b] = []
-            part = POS // PACK
             for start in range(first, POS, BANK_COLS):
                 stop = min(start + BANK_COLS, POS)
                 regrouped = psum.tile([P, stop - start, PACK], BF16)
-                for c in range(start, stop, part):
-                    end = min(c + part, stop)
+                for pair in range(0, PACK, 2):
                     nc.tensor.matmul(
-                        regrouped[:, c - start : end - start, :].rearrange("p c j -> p j c"),
+                        regrouped[:, :, pair : pair + 2],
                         lhsT=identity[:],
-                        rhs=h_rows[b][:, :, c:end],
+                        rhs=h_rows[b][:, pair : pair + 2, start:stop].rearrange("p j c -> p c j"),
                         start=True,
                         stop=True,
                     )

@@ -414,7 +414,6 @@ def tile_bottleneck_transformer_pb_t_kernel(
                 quantise_x(b, [1])
             else:
                 quantise_x(b, [0, 1])
-            rectify(b - 1)
             scale_main(b)
             if not last:
                 copy_h_banks(b + 1)
@@ -423,5 +422,6 @@ def tile_bottleneck_transformer_pb_t_kernel(
             if b + 2 < BATCH:
                 regroup_h_on_tensor(b + 2, H_GPSIMD)
                 regroup_h_on_gpsimd(b + 2)
+            rectify(b - 1)
             add_short(b)
         rectify_last(BATCH - 1)

@@ -29,12 +29,14 @@ FLOPS = 2 * BATCH * C_OUT * (C_MAIN + C_SHORT) * POS
 
 RUN = 8
 HEAD_BATCHES = 2
-HEAD_SCALAR = 304
+HEAD_SCALAR = 296
 H2_SCALAR = 48
 H2_VECTOR = 208
 X_SCALAR = 296
-H_GPSIMD = 160
+H_GPSIMD = 168
+H_TENSOR_FIRST = H_GPSIMD - 1
 BANK_COLS = 256
+ROW_PAD = 16
 LOOKAHEAD = 6
 
 
@@ -300,10 +302,10 @@ def tile_bottleneck_transformer_pb_t_kernel(
             scaled_of[b] = scaled_main
 
         def add_short(b):
-            summed = result.tile([P, M_TILES, POS], F32)
+            summed = result.tile([P, M_TILES, POS + ROW_PAD], F32)
             for m in range(M_TILES):
                 nc.vector.scalar_tensor_tensor(
-                    out=summed[:, m, :],
+                    out=summed[:, m, 0:POS],
                     in0=short_of[b][m][:],
                     scalar=scale[:, M_TILES + m : M_TILES + m + 1],
                     in1=scaled_of[b][:, m, :],
@@ -313,12 +315,12 @@ def tile_bottleneck_transformer_pb_t_kernel(
             summed_of[b] = summed
 
         def rectify(b):
-            rectified = stored.tile([P, M_TILES, POS], F32)
+            rectified = stored.tile([P, M_TILES, POS + ROW_PAD], F32)
             if b < HEAD_BATCHES:
                 for m in range(M_TILES):
                     nc.vector.tensor_scalar(
-                        out=rectified[:, m, :],
-                        in0=summed_of[b][:, m, :],
+                        out=rectified[:, m, 0:POS],
+                        in0=summed_of[b][:, m, 0:POS],
                         scalar1=offset[:, m : m + 1],
                         scalar2=0.0,
                         op0=ALU.add,
@@ -326,24 +328,24 @@ def tile_bottleneck_transformer_pb_t_kernel(
                     )
             else:
                 nc.vector.tensor_scalar_max(
-                    out=rectified[:].rearrange("p m w -> p (m w)"),
-                    in0=summed_of[b][:].rearrange("p m w -> p (m w)"),
-                    scalar1=0.0,
+                    out=rectified[:, :, 0:POS], in0=summed_of[b][:, :, 0:POS], scalar1=0.0
                 )
-            nc.sync.dma_start(out=out[b].rearrange("(m p) w -> p m w", p=P), in_=rectified[:])
+            nc.sync.dma_start(
+                out=out[b].rearrange("(m p) w -> p m w", p=P), in_=rectified[:, :, 0:POS]
+            )
 
         def rectify_last(b):
-            rectified = stored.tile([P, M_TILES, POS], F32)
+            rectified = stored.tile([P, M_TILES, POS + ROW_PAD], F32)
             for m in range(M_TILES):
                 if m == 0:
                     nc.scalar.activation(
-                        out=rectified[:, m, :], in_=summed_of[b][:, m, :], func=ACT.Relu
+                        out=rectified[:, m, 0:POS], in_=summed_of[b][:, m, 0:POS], func=ACT.Relu
                     )
                 else:
                     nc.vector.tensor_scalar_max(
-                        out=rectified[:, m, :], in0=summed_of[b][:, m, :], scalar1=0.0
+                        out=rectified[:, m, 0:POS], in0=summed_of[b][:, m, 0:POS], scalar1=0.0
                     )
-                nc.sync.dma_start(out=out[b, P * m : P * (m + 1), :], in_=rectified[:, m, :])
+                nc.sync.dma_start(out=out[b, P * m : P * (m + 1), :], in_=rectified[:, m, 0:POS])
 
         def load(b):
             if b < BATCH:
@@ -401,7 +403,7 @@ def tile_bottleneck_transformer_pb_t_kernel(
         fold_offsets()
         regroup_x(2)
         quantise_h(2)
-        regroup_h_on_tensor(3, H_GPSIMD)
+        regroup_h_on_tensor(3, H_TENSOR_FIRST)
         regroup_h_on_gpsimd(3)
         add_short(1)
         rectify(0)
@@ -420,7 +422,7 @@ def tile_bottleneck_transformer_pb_t_kernel(
                 regroup_x(b + 1)
                 quantise_h(b + 1)
             if b + 2 < BATCH:
-                regroup_h_on_tensor(b + 2, H_GPSIMD)
+                regroup_h_on_tensor(b + 2, H_TENSOR_FIRST)
                 regroup_h_on_gpsimd(b + 2)
             rectify(b - 1)
             add_short(b)

from contextlib import ExitStack

import concourse.mybir as mybir
from concourse.masks import make_identity

F32 = mybir.dt.float32
BF16 = mybir.dt.bfloat16
I32 = mybir.dt.int32
U32 = mybir.dt.uint32
U8 = mybir.dt.uint8
FP8X4 = mybir.dt.float8_e4m3fn_x4
FP4X4 = mybir.dt.float4_e2m1fn_x4
ALU = mybir.AluOpType
ACT = mybir.ActivationFunctionType

P = 128
PACK = 4
BATCH = 16
C_MAIN = 512
C_SHORT = 1024
C_OUT = 256
M_TILES = C_OUT // P
POS = 512
X_PASSES = C_SHORT // (P * PACK)
PASSES = 1 + X_PASSES
EPS = 1e-5

FLOPS = 2 * BATCH * C_OUT * (C_MAIN + C_SHORT) * POS

RUN = 8
HEAD_BATCHES = 2
HEAD_SCALAR = 296
H2_SCALAR = 48
H2_VECTOR = 208
X_SCALAR = 296
H_GPSIMD = 168
H_TENSOR_FIRST = H_GPSIMD - 1
BANK_COLS = 256
ROW_PAD = 16
LOOKAHEAD = 6


def tile_bottleneck_transformer_pb_t_kernel(
    tc,
    h_attn,
    x,
    conv3_w_words,
    conv3_w_scales,
    bn3_g,
    bn3_b,
    bn3_m,
    bn3_v,
    sc_w_words,
    sc_w_scales,
    sc_b,
    scbn_g,
    scbn_b,
    scbn_m,
    scbn_v,
    out,
):
    nc = tc.nc
    with ExitStack() as ctx:
        ctx.enter_context(tc.manual_schedule())
        const = ctx.enter_context(tc.tile_pool(name="const", bufs=1))
        raw = ctx.enter_context(tc.tile_pool(name="raw", bufs=LOOKAHEAD + 1))
        stage = ctx.enter_context(tc.tile_pool(name="stage", bufs=3))
        quantised = ctx.enter_context(tc.tile_pool(name="quantised", bufs=3))
        result = ctx.enter_context(tc.tile_pool(name="result", bufs=2))
        stored = ctx.enter_context(tc.tile_pool(name="stored", bufs=12))
        psum_main = ctx.enter_context(tc.psum_pool(name="psum_main", bufs=1))
        psum = ctx.enter_context(tc.psum_pool(name="psum", bufs=2))

        w_words = const.tile([P, PASSES, 2 * C_OUT], U8, align_bytes=64)
        w_scales = const.tile([P, PASSES, C_OUT], U8, align_bytes=64)
        scale_rows = const.tile([P, P], BF16)
        nc.vector.memset(scale_rows[:], 0.0)
        offset_rows = const.tile([P, P], BF16)
        nc.vector.memset(offset_rows[:], 0.0)
        nc.vector.memset(w_scales[:].rearrange("p s n -> p (s n)").bitcast(I32), 0)

        def load_words(words, first_pass, passes):
            mine = slice(first_pass, first_pass + passes)
            nc.sync.dma_start(
                out=w_words[:, mine, :].bitcast(I32),
                in_=words.rearrange("g p n -> p g n").bitcast(I32),
            )

        def load_scales(scales, first_pass, passes):
            mine = slice(first_pass, first_pass + passes)
            for quadrant in range(4):
                nc.sync.dma_start(
                    out=w_scales[32 * quadrant : 32 * quadrant + 4, mine, :].bitcast(I32),
                    in_=scales[:, 4 * quadrant : 4 * quadrant + 4, :]
                    .rearrange("g r n -> r g n")
                    .bitcast(I32),
                )

        h_rows = {}
        x_rows = {}
        h_grouped = {}
        x_grouped = {}
        h_banks = {}
        main_of = {}
        short_of = {}
        scaled_of = {}
        summed_of = {}

        def load_h(b):
            h_raw = raw.tile([P, PACK, POS], BF16)
            nc.sync.dma_start(out=h_raw[:], in_=h_attn[b].rearrange("(p j) w -> p j w", j=PACK))
            h_rows[b] = h_raw

        def load_x(b):
            x_raw = raw.tile([P, X_PASSES, PACK, POS], BF16)
            x_rows[b] = x_raw
            rows = x[b].rearrange("(g p j) w -> p g j w", p=P, j=PACK)
            if b < HEAD_BATCHES:
                return [
                    lambda g=g: nc.sync.dma_start(out=x_raw[:, g], in_=rows[:, g])
                    for g in range(X_PASSES)
                ]
            nc.sync.dma_start(out=x_raw[:], in_=rows)
            return []

        scale_vectors = [bn3_v, scbn_v, bn3_g, scbn_g]
        offset_vectors = [bn3_m, scbn_m, bn3_b, scbn_b, sc_b]

        def load_vectors(queue, rows, vectors):
            for v, vector in enumerate(vectors):
                queue.dma_start(
                    out=rows[M_TILES * v : M_TILES * (v + 1), :],
                    in_=vector.rearrange("(m c) -> m c", m=M_TILES),
                )

        identity = const.tile([P, P], BF16)
        make_identity(nc, identity[:])
        load_vectors(nc.gpsimd, offset_rows, offset_vectors)

        ones = const.tile([P, 1], F32)
        nc.vector.memset(ones[:], 1.0)
        warm = const.tile([P, 1], F32)
        nc.scalar.activation(out=warm[:], in_=ones[:], func=ACT.Sqrt)

        scale = const.tile([P, 2 * M_TILES], F32)
        offset = const.tile([P, M_TILES], F32)
        gains = const.tile([P, 8], F32)
        std = const.tile([P, 4], F32)
        rstd = const.tile([P, 4], F32)

        def fold_variances():
            nc.vector.tensor_copy(out=gains[:], in_=cols_ps[:, 0:8])
            var_eps = const.tile([P, 4], F32)
            nc.vector.tensor_scalar_add(out=var_eps[:], in0=gains[:, 0:4], scalar1=EPS)
            nc.scalar.activation(out=std[:], in_=var_eps[:], func=ACT.Sqrt)

        def fold_scales():
            nc.vector.reciprocal(out=rstd[:], in_=std[:])
            nc.vector.tensor_mul(out=scale[:], in0=gains[:, 4:8], in1=rstd[:])

        def fold_offsets():
            shifts = const.tile([P, 10], F32)
            nc.vector.tensor_copy(out=shifts[:], in_=cols_ps[:, P : P + 10])
            mean, shift, bias = shifts[:, 0:4], shifts[:, 4:8], shifts[:, 8:10]
            centre = const.tile([P, 4], F32)
            nc.gpsimd.tensor_copy(out=centre[:, 0:2], in_=mean[:, 0:2])
            nc.gpsimd.tensor_sub(out=centre[:, 2:4], in0=mean[:, 2:4], in1=bias)
            scaled_centre = const.tile([P, 4], F32)
            nc.gpsimd.tensor_mul(out=scaled_centre[:], in0=centre[:], in1=scale[:])
            both = const.tile([P, 4], F32)
            nc.gpsimd.tensor_sub(out=both[:], in0=shift, in1=scaled_centre[:])
            nc.gpsimd.tensor_add(out=offset[:], in0=both[:, 0:2], in1=both[:, 2:4])

        def interleave(copy, grouped, rows, cols):
            if len(rows.shape) == 4:
                copy(
                    out=grouped[:, :, cols, :].rearrange("p g (c i) j -> p g c j i", i=RUN),
                    in_=rows[:, :, :, cols].rearrange("p g j (c i) -> p g c j i", i=RUN),
                )
            else:
                copy(
                    out=grouped[:, cols, :].rearrange("p (c i) j -> p c j i", i=RUN),
                    in_=rows[:, :, cols].rearrange("p j (c i) -> p c j i", i=RUN),
                )

        def regroup_h_on_tensor(b, first):
            h_banks[b] = []
            for start in range(first, POS, BANK_COLS):
                stop = min(start + BANK_COLS, POS)
                regrouped = psum.tile([P, stop - start, PACK], BF16)
                for pair in range(0, PACK, 2):
                    nc.tensor.matmul(
                        regrouped[:, :, pair : pair + 2],
                        lhsT=identity[:],
                        rhs=h_rows[b][:, pair : pair + 2, start:stop].rearrange("p j c -> p c j"),
                        start=True,
                        stop=True,
                    )
                h_banks[b].append((slice(start, stop), regrouped))

        def copy_h_banks(b):
            for cols, regrouped in h_banks[b]:
                nc.scalar.copy(out=h_grouped[b][:, cols, :], in_=regrouped[:])

        def regroup_h_on_gpsimd(b):
            early = stage.tile([P, POS, PACK], BF16, align_bytes=64, bufs=1)
            cols = slice(0, H_GPSIMD)
            nc.gpsimd.tensor_scalar(
                out=early[:, cols, :],
                in0=h_rows[b][:, :, cols].rearrange("p j c -> p c j"),
                scalar1=1.0,
                scalar2=0.0,
                op0=ALU.mult,
                op1=ALU.add,
            )
            h_grouped[b] = early

        def regroup_head_h(b, scalar_cols, vector_cols):
            grouped_h = stage.tile([P, POS, PACK], BF16, align_bytes=64)
            h_grouped[b] = grouped_h
            interleave(nc.vector.tensor_copy, grouped_h, h_rows[b], vector_cols)
            interleave(nc.scalar.copy, grouped_h, h_rows[b], scalar_cols)

        def new_x(b):
            grouped_x = stage.tile([P, X_PASSES, POS, PACK], BF16, align_bytes=64)
            x_grouped[b] = grouped_x

        def regroup_x_pass(b, g, split):
            if g == 0:
                new_x(b)
            for copy, cols in (
                (nc.vector.tensor_copy, slice(split, POS)),
                (nc.scalar.copy, slice(0, split)),
            ):
                interleave(copy, x_grouped[b][:, g], x_rows[b][:, g], cols)

        def regroup_x(b):
            new_x(b)
            interleave(nc.vector.tensor_copy, x_grouped[b], x_rows[b], slice(X_SCALAR, POS))
            interleave(nc.scalar.copy, x_grouped[b], x_rows[b], slice(0, X_SCALAR))

        def multiply(s, codes, scales, accs):
            for m in range(M_TILES):
                nc.tensor.matmul_mx(
                    out=accs[m][:],
                    lhsT=w_words[:, s, 2 * P * m : 2 * P * (m + 1)].bitcast(FP4X4),
                    lhsT_scale=w_scales[:, s, P * m : P * (m + 1)],
                    rhs=codes.bitcast(FP8X4),
                    rhs_scale=scales,
                    start=(s != PASSES - 1),
                    stop=(s != 1),
                )

        def quantise_h(b):
            h_codes = quantised.tile([P, POS], U32, align_bytes=64)
            h_scales = quantised.tile([P, POS], U8, align_bytes=64)
            nc.vector.quantize_mx(
                out=h_codes[:].bitcast(FP8X4),
                scales=h_scales[:],
                in_=h_grouped[b][:].rearrange("p w j -> p (w j)"),
            )
            main_of[b] = [
                psum.tile([P, POS], F32, name="first%d" % m, tag="short%d" % m)
                if b == 0
                else psum_main.tile([P, POS], F32, name="main%d" % m)
                for m in range(M_TILES)
            ]
            multiply(0, h_codes[:], h_scales[:], main_of[b])

        def quantise_x(b, passes):
            if passes[0] == 0:
                short_of[b] = [psum.tile([P, POS], F32, name="short%d" % m) for m in range(M_TILES)]
            n = len(passes)
            x_codes = quantised.tile([P, X_PASSES, POS], U32, align_bytes=64)
            x_scales = quantised.tile([P, X_PASSES, POS], U8, align_bytes=64)
            nc.vector.quantize_mx(
                out=x_codes[:, 0:n].rearrange("p g w -> p (g w)").bitcast(FP8X4),
                scales=x_scales[:, 0:n].rearrange("p g w -> p (g w)"),
                in_=x_grouped[b][:, passes[0] : passes[0] + n].rearrange("p g w j -> p (g w j)"),
            )
            for i, g in enumerate(passes):
                multiply(1 + g, x_codes[:, i, :], x_scales[:, i, :], short_of[b])

        def scale_main(b):
            scaled_main = result.tile([P, M_TILES, POS], F32)
            for m in range(M_TILES):
                if b < HEAD_BATCHES:
                    nc.scalar.activation(
                        out=scaled_main[:, m, :],
                        in_=main_of[b][m][:],
                        func=ACT.Copy,
                        scale=scale[:, m : m + 1],
                    )
                else:
                    nc.scalar.activation(
                        out=scaled_main[:, m, :],
                        in_=main_of[b][m][:],
                        func=ACT.Identity,
                        scale=scale[:, m : m + 1],
                        bias=offset[:, m : m + 1],
                    )
            scaled_of[b] = scaled_main

        def add_short(b):
            summed = result.tile([P, M_TILES, POS + ROW_PAD], F32)
            for m in range(M_TILES):
                nc.vector.scalar_tensor_tensor(
                    out=summed[:, m, 0:POS],
                    in0=short_of[b][m][:],
                    scalar=scale[:, M_TILES + m : M_TILES + m + 1],
                    in1=scaled_of[b][:, m, :],
                    op0=ALU.mult,
                    op1=ALU.add,
                )
            summed_of[b] = summed

        def rectify(b):
            rectified = stored.tile([P, M_TILES, POS + ROW_PAD], F32)
            if b < HEAD_BATCHES:
                for m in range(M_TILES):
                    nc.vector.tensor_scalar(
                        out=rectified[:, m, 0:POS],
                        in0=summed_of[b][:, m, 0:POS],
                        scalar1=offset[:, m : m + 1],
                        scalar2=0.0,
                        op0=ALU.add,
                        op1=ALU.max,
                    )
            else:
                nc.vector.tensor_scalar_max(
                    out=rectified[:, :, 0:POS], in0=summed_of[b][:, :, 0:POS], scalar1=0.0
                )
            nc.sync.dma_start(
                out=out[b].rearrange("(m p) w -> p m w", p=P), in_=rectified[:, :, 0:POS]
            )

        def rectify_last(b):
            rectified = stored.tile([P, M_TILES, POS + ROW_PAD], F32)
            for m in range(M_TILES):
                if m == 0:
                    nc.scalar.activation(
                        out=rectified[:, m, 0:POS], in_=summed_of[b][:, m, 0:POS], func=ACT.Relu
                    )
                else:
                    nc.vector.tensor_scalar_max(
                        out=rectified[:, m, 0:POS], in0=summed_of[b][:, m, 0:POS], scalar1=0.0
                    )
                nc.sync.dma_start(out=out[b, P * m : P * (m + 1), :], in_=rectified[:, m, 0:POS])

        def load(b):
            if b < BATCH:
                load_h(b)
                for load_piece in load_x(b):
                    load_piece()

        load_h(0)
        load_words(conv3_w_words, 0, 1)
        load_scales(conv3_w_scales, 0, 1)
        x0_pass1, x0_pass2 = load_x(0)
        x0_pass1()
        x0_pass2()
        load_vectors(nc.sync, scale_rows, scale_vectors)
        load_h(1)
        load_words(sc_w_words, 1, 2)
        x1_pass1, x1_pass2 = load_x(1)
        x1_pass1()
        load_scales(sc_w_scales, 1, 2)
        x1_pass2()
        for b in range(2, LOOKAHEAD):
            load_h(b)
            for load in load_x(b):
                load()

        cols_ps = psum.tile([P, 2 * P], BF16, tag="regrouped")

        head_split = HEAD_SCALAR
        scalar_cols, vector_cols = slice(0, head_split), slice(head_split, POS)
        regroup_head_h(0, scalar_cols, vector_cols)
        load(LOOKAHEAD)
        regroup_x_pass(0, 0, head_split)
        quantise_h(0)
        nc.tensor.transpose(cols_ps[:, 0:P], scale_rows[:], identity[:])
        regroup_x_pass(0, 1, head_split)
        quantise_x(0, [0])
        regroup_head_h(1, scalar_cols, vector_cols)
        load(1 + LOOKAHEAD)
        quantise_x(0, [1])
        fold_variances()
        regroup_x_pass(1, 0, head_split)
        quantise_h(1)
        regroup_h_on_tensor(2, H2_SCALAR + H2_VECTOR)
        fold_scales()
        regroup_x_pass(1, 1, head_split)
        scale_main(0)
        scale_main(1)
        quantise_x(1, [0])
        nc.tensor.transpose(cols_ps[:, P : 2 * P], offset_rows[:], identity[:])
        regroup_head_h(2, slice(0, H2_SCALAR), slice(H2_SCALAR, H2_SCALAR + H2_VECTOR))
        copy_h_banks(2)
        load(2 + LOOKAHEAD)
        quantise_x(1, [1])
        add_short(0)
        fold_offsets()
        regroup_x(2)
        quantise_h(2)
        regroup_h_on_tensor(3, H_TENSOR_FIRST)
        regroup_h_on_gpsimd(3)
        add_short(1)
        rectify(0)

        for b in range(HEAD_BATCHES, BATCH):
            last = b == BATCH - 1
            load(b + 1 + LOOKAHEAD)
            if last:
                quantise_x(b, [0])
                quantise_x(b, [1])
            else:
                quantise_x(b, [0, 1])
            scale_main(b)
            if not last:
                copy_h_banks(b + 1)
                regroup_x(b + 1)
                quantise_h(b + 1)
            if b + 2 < BATCH:
                regroup_h_on_tensor(b + 2, H_TENSOR_FIRST)
                regroup_h_on_gpsimd(b + 2)
            rectify(b - 1)
            add_short(b)
        rectify_last(BATCH - 1)
